import numpy as np
import ml_dtypes


def mxq(x, axis, fmt="e4m3"):
    dtype, down = {"e4m3": (ml_dtypes.float8_e4m3fn, 7), "e5m2": (ml_dtypes.float8_e5m2, 14)}[fmt]
    v = np.moveaxis(np.asarray(x, np.float32).astype(ml_dtypes.bfloat16).astype(np.float64), axis, -1)
    blocks = v.reshape(v.shape[:-1] + (-1, 32))
    amax = np.abs(blocks).max(-1, keepdims=True)
    byte = np.maximum(np.where(amax > 0, np.frexp(amax)[1] - 1 + 127, 0) - down, 1)
    scale = np.exp2(byte - 127.0)
    codes = (blocks / scale).astype(np.float32).astype(dtype).astype(np.float64)
    return np.moveaxis((codes * scale).reshape(v.shape), -1, axis)


WIDE = False


def mx_kscale(k):
    if not WIDE:
        return np.ones(k)
    levels = np.array([10, -10, 5, -5, 0])
    a = np.random.permutation(np.resize(levels, k // 512 * 4)).reshape(k // 512, 4)
    idx = np.arange(k)
    return np.exp2(a[idx // 512, idx % 128 // 32])


BF16 = ml_dtypes.bfloat16


def bf(x):
    return np.asarray(x, np.float32).astype(BF16)


def f64(x):
    return np.asarray(x).astype(np.float64)


E2M1 = np.array([0.0, 0.5, 1.0, 1.5, 2.0, 3.0, 4.0, 6.0, -0.0, -0.5, -1.0, -1.5, -2.0, -3.0, -4.0, -6.0])


def pack_weight(w, fmt):
    k, n = w.shape
    w = f64(bf(w)).reshape(k // 32, 32, n)
    amax = np.abs(w).max(1)
    if fmt == "e4m3":
        byte = np.frexp(amax)[1] - 1 + 127 - 7
    else:
        mant, ex = np.frexp(amax / 6.0)
        byte = np.where(mant > 0.5, ex, ex - 1) + 127
    byte = np.clip(np.where(amax > 0, byte, 1), 1, 254)
    scaled = (w * np.exp2(127.0 - byte)[:, None, :]).reshape(k, n).astype(np.float32)
    by_word = np.ascontiguousarray(scaled.reshape(k // 512, 128, 4, n).transpose(0, 1, 3, 2))
    if fmt == "e4m3":
        words = by_word.astype(ml_dtypes.float8_e4m3fn).view(np.uint8)
    else:
        c = by_word.astype(ml_dtypes.float4_e2m1fn).view(np.uint8) & 0xF
        words = c[..., 0::2] | (c[..., 1::2] << 4)
    return np.ascontiguousarray(words), np.ascontiguousarray(byte.astype(np.uint8).reshape(k // 512, 16, n))


def unpack_weight(words, scales, fmt):
    g, p, n, _ = words.shape
    if fmt == "e4m3":
        vals = np.ascontiguousarray(words).view(ml_dtypes.float8_e4m3fn).astype(np.float64)
    else:
        nib = np.empty((g, p, n, 4), np.uint8)
        nib[..., 0::2] = words & 0xF
        nib[..., 1::2] = words >> 4
        vals = E2M1[nib]
    vals = vals * np.repeat(np.exp2(scales.astype(np.float64) - 127.0), 8, axis=1)[..., None]
    return vals.transpose(0, 1, 3, 2).reshape(g * 512, n)

def pack4(w):
    words, scales = pack_weight(w, "e2m1")
    return words.reshape(words.shape[0], 128, -1), scales


def unpack4(words, scales):
    return unpack_weight(words.reshape(words.shape[0], 128, -1, 2), scales, "e2m1")


B, K, L, D, H = 8, 8, 512, 256, 128


def erf(v):
    c = np.clip(v, -6.0, 6.0)
    q = 2.0 * c * c
    term = c.copy()
    total = c.copy()
    for n in range(1, 120):
        term = term * q / (2.0 * n + 1.0)
        total = total + term
    return 2.0 / np.sqrt(np.pi) * np.exp(-c * c) * total


def gelu_erf(v):
    return 0.5 * v * (1.0 + erf(v / np.sqrt(2.0)))


def sigmoid(v):
    return 1.0 / (1.0 + np.exp(-v))


def setup_inputs():
    t = mx_kscale(2 * D)[D:]
    wf = np.random.standard_normal((2 * D, D)) / np.sqrt(2 * D)
    wf[D:] = wf[D:] / t[:, None]
    wf_words, wf_scales = pack4(wf)
    return {
        "orig_feat": bf(np.random.standard_normal((B, L, D))),
        "rag_feat": bf(np.random.standard_normal((B, K, L, D)) * t),
        "af": bf(np.random.uniform(0.01, 0.99, (B, L))),
        "h_af": bf(np.maximum(np.random.standard_normal((B, L, H)), 0.0) * np.random.uniform(0.0, 1.0, (B, L, 1))),
        "w2": bf(np.random.standard_normal((H, D)) * 2.0 / np.sqrt(H)),
        "b2": bf(-np.log(D / 2.0) + 0.3 * np.random.standard_normal(D)),
        "wf_words": wf_words,
        "wf_scales": wf_scales,
        "bias_f": bf(np.random.standard_normal(D) * 0.5),
        "ln_g": bf(1.0 + 0.2 * np.random.standard_normal(D)),
        "ln_b": bf(0.3 * np.random.standard_normal(D)),
    }


def reference(orig_feat, rag_feat, af, h_af, w2, b2, wf_words, wf_scales, bias_f, ln_g, ln_b):
    o, r, a = f64(orig_feat), f64(rag_feat), f64(af)
    af_weight = sigmoid(f64(h_af) @ f64(w2) + f64(b2))
    s = af_weight.sum(-1)
    pooled_ref = (0.7 * r.mean(axis=1) + 0.3 * r.max(axis=1)) * s[:, :, None]
    x = np.concatenate([o, pooled_ref], axis=-1)
    y = (mxq(x, 2, "e4m3") @ unpack4(wf_words, wf_scales)) + f64(bias_f)
    mu = y.mean(-1, keepdims=True)
    var = ((y - mu) ** 2).mean(-1, keepdims=True)
    yn = (y - mu) / np.sqrt(var + 1e-5) * f64(ln_g) + f64(ln_b)
    fused = gelu_erf(yn)
    return o + fused * np.sqrt(a * (1.0 - a))[..., None]

@@ -1,0 +1,290 @@
+from contextlib import ExitStack
+
+import concourse.mybir as mybir
+from concourse.masks import make_identity
+
+F32 = mybir.dt.float32
+BF16 = mybir.dt.bfloat16
+I32 = mybir.dt.int32
+U32 = mybir.dt.uint32
+U8 = mybir.dt.uint8
+FP8X4 = mybir.dt.float8_e4m3fn_x4
+FP4X4 = mybir.dt.float4_e2m1fn_x4
+ACT = mybir.ActivationFunctionType
+ALU = mybir.AluOpType
+
+P = 128
+B, REFS, L, D, H = 8, 8, 512, 256, 128
+J = 2
+UNIT = P * J
+UNITS = B * L // UNIT
+UNITS_PER_BATCH = L // UNIT
+HALVES = D // P
+PACK = 4
+WORDS = 2
+K = 2 * D
+
+MEAN_WEIGHT = 0.7 / REFS
+MAX_WEIGHT = 0.3
+LN_EPS = 1e-5
+
+PREFETCH = 3
+
+FLOPS = 2 * B * L * K * D + 2 * B * L * H * D
+
+
+def tile_rarevariantawarefusion_pa_t_kernel(
+    tc, orig_feat, rag_feat, af, h_af, w2, b2, wf_words, wf_scales, bias_f, ln_g, ln_b, out
+):
+    nc = tc.nc
+
+    orig_units = orig_feat.flatten_outer_dims().rearrange("(u p j) d -> u p j d", p=P, j=J)
+    out_units = out.flatten_outer_dims().rearrange("(u p j) d -> u p (j d)", p=P, j=J)
+
+    with ExitStack() as ctx:
+        const = ctx.enter_context(tc.tile_pool(name="const", bufs=1))
+        rag_pool = ctx.enter_context(tc.tile_pool(name="rag", bufs=PREFETCH + 1))
+        x_pool = ctx.enter_context(tc.tile_pool(name="x", bufs=PREFETCH + 4))
+        tree = ctx.enter_context(tc.tile_pool(name="tree", bufs=2))
+        q_pool = ctx.enter_context(tc.tile_pool(name="q", bufs=5))
+        work = ctx.enter_context(tc.tile_pool(name="work", bufs=3))
+        stats = ctx.enter_context(tc.tile_pool(name="stats", bufs=4))
+
+        rag_of = {}
+        x_of = {}
+
+        def load_unit(u):
+            b, first = u // UNITS_PER_BATCH, (u % UNITS_PER_BATCH) * UNIT
+            rag = rag_pool.tile([P, REFS, J * D], BF16)
+            nc.sync.dma_start(
+                out=rag[:], in_=rag_feat[b, :, first : first + UNIT, :].rearrange("k (p j) d -> p k (j d)", j=J)
+            )
+            x = x_pool.tile([P, J, K], BF16)
+            nc.sync.dma_start(out=x[:, :, 0:D], in_=orig_units[u])
+            rag_of[u] = rag
+            x_of[u] = x
+
+        load_unit(0)
+
+        ident_f = const.tile([P, P], F32)
+        make_identity(nc, ident_f[:])
+        ident_b = const.tile([P, P], BF16)
+        make_identity(nc, ident_b[:])
+
+        h_all = const.tile([P, UNITS, J * H], BF16)
+        nc.sync.dma_start(out=h_all[:], in_=h_af.flatten_outer_dims().rearrange("(u p j) h -> p u (j h)", p=P, j=J))
+        w2_sb = const.tile([H, D], BF16)
+        nc.sync.dma_start(out=w2_sb[:], in_=w2)
+
+        vec_rows = const.tile([P, P], BF16)
+        nc.gpsimd.memset(vec_rows[:], 0.0)
+        B2, BIAS_F, LN_G, LN_B = 0, 2, 4, 6
+        for first_row, vec in ((B2, b2), (BIAS_F, bias_f), (LN_G, ln_g), (LN_B, ln_b)):
+            nc.sync.dma_start(
+                out=vec_rows[first_row : first_row + HALVES, :], in_=vec.rearrange("(h n) -> h n", h=HALVES)
+            )
+
+        wf_sb = const.tile([P, 2 * D], U8, align_bytes=64)
+        nc.sync.dma_start(out=wf_sb[:].bitcast(I32), in_=wf_words[0].bitcast(I32))
+        wf_plane = const.tile([P, D], U8, align_bytes=64)
+        nc.vector.memset(wf_plane[:].bitcast(I32), 0)
+        for quad in range(4):
+            nc.sync.dma_start(
+                out=wf_plane[32 * quad : 32 * quad + 4, :].bitcast(I32),
+                in_=wf_scales[0, 4 * quad : 4 * quad + 4, :].bitcast(I32),
+            )
+
+        af_sb = const.tile([P, UNITS, J], BF16)
+        nc.sync.dma_start(out=af_sb[:], in_=af.rearrange("b l -> (b l)").rearrange("(u p j) -> p u j", p=P, j=J))
+
+        for u in range(1, PREFETCH):
+            load_unit(u)
+
+        half = const.tile([P, UNITS * J], F32)
+        nc.gpsimd.memset(half[:], 0.5)
+        minus_half = const.tile([P, J], F32)
+        nc.gpsimd.memset(minus_half[:], -0.5)
+        af_flat = af_sb[:].rearrange("p u j -> p (u j)")
+        one_minus_af = const.tile([P, UNITS * J], F32)
+        nc.gpsimd.tensor_scalar(out=one_minus_af[:], in0=af_flat, scalar1=-1.0, scalar2=1.0, op0=ALU.mult, op1=ALU.add)
+        af_product = const.tile([P, UNITS * J], F32)
+        nc.gpsimd.tensor_tensor(out=af_product[:], in0=one_minus_af[:], in1=af_flat, op=ALU.mult)
+        af_factor = const.tile([P, UNITS * J], F32)
+        nc.gpsimd.tensor_tensor(out=af_factor[:], in0=af_product[:], in1=half[:], op=ALU.pow)
+
+        vec_cols = const.tile([P, 4 * HALVES], F32)
+        gate = const.tile([P, UNITS * J], F32)
+        CHUNK = 2
+        with tc.psum_pool(name="gate_psum", bufs=2) as gate_psum, tc.tile_pool(name="gate_sbuf", bufs=2) as gate_sbuf:
+            vec_ps = gate_psum.tile([P, CHUNK * UNIT], BF16, tag="hT_ps")
+            nc.tensor.transpose(out=vec_ps[:, 0:P], in_=vec_rows[:], identity=ident_b[:])
+            nc.scalar.copy(out=vec_cols[:], in_=vec_ps[:, 0 : 4 * HALVES])
+
+            for c in range(UNITS // CHUNK):
+                hT_ps = gate_psum.tile([P, CHUNK * UNIT], BF16, tag="hT_ps")
+                for blk in range(CHUNK * J):
+                    u, j = CHUNK * c + blk // J, blk % J
+                    nc.tensor.transpose(
+                        out=hT_ps[:, blk * P : (blk + 1) * P], in_=h_all[:, u, j * H : (j + 1) * H], identity=ident_b[:]
+                    )
+                hT = gate_sbuf.tile([P, CHUNK * UNIT], BF16)
+                nc.scalar.copy(out=hT[:], in_=hT_ps[:])
+                sigT = gate_sbuf.tile([P, HALVES, CHUNK * UNIT], F32)
+                for h in range(HALVES):
+                    logits = gate_psum.tile([P, CHUNK * UNIT], F32, tag="logits")
+                    nc.tensor.matmul(out=logits[:], lhsT=w2_sb[:, h * P : (h + 1) * P], rhs=hT[:], start=True, stop=True)
+                    nc.scalar.activation(
+                        out=sigT[:, h, :], in_=logits[:], func=ACT.Sigmoid, bias=vec_cols[:, B2 + h : B2 + h + 1]
+                    )
+                for uu in range(CHUNK):
+                    sig_ps = gate_psum.tile([P, J, D], F32, tag="sig_ps")
+                    for j in range(J):
+                        blk = uu * J + j
+                        for h in range(HALVES):
+                            nc.tensor.transpose(
+                                out=sig_ps[:, j, h * P : (h + 1) * P],
+                                in_=sigT[:, h, blk * P : (blk + 1) * P],
+                                identity=ident_f[:],
+                            )
+                    for j in range(J):
+                        col = (CHUNK * c + uu) * J + j
+                        unused = gate_sbuf.tile([P, D], BF16, tag="unused")
+                        nc.scalar.activation(
+                            out=unused[:],
+                            in_=sig_ps[:, j, :],
+                            func=ACT.Identity,
+                            scale=MEAN_WEIGHT,
+                            accum_out=gate[:, col : col + 1],
+                        )
+
+        psum = ctx.enter_context(tc.psum_pool(name="psum", bufs=1))
+
+        for u in range(UNITS):
+            if u + PREFETCH < UNITS:
+                load_unit(u + PREFETCH)
+            rag, x = rag_of[u], x_of[u]
+
+            max4 = tree.tile([P, 4, J * D], BF16)
+            nc.vector.tensor_tensor(out=max4[:], in0=rag[:, 0:4, :], in1=rag[:, 4:8, :], op=ALU.max)
+            sum4 = tree.tile([P, 4, J * D], F32)
+            nc.vector.tensor_tensor(out=sum4[:], in0=rag[:, 0:4, :], in1=rag[:, 4:8, :], op=ALU.add)
+            max2 = tree.tile([P, 2, J * D], BF16)
+            nc.vector.tensor_tensor(out=max2[:], in0=max4[:, 0:2, :], in1=max4[:, 2:4, :], op=ALU.max)
+            sum2 = tree.tile([P, 2, J * D], F32)
+            nc.vector.tensor_tensor(out=sum2[:], in0=sum4[:, 0:2, :], in1=sum4[:, 2:4, :], op=ALU.add)
+            max1 = tree.tile([P, J * D], BF16)
+            nc.vector.tensor_tensor(out=max1[:], in0=max2[:, 0, :], in1=max2[:, 1, :], op=ALU.max)
+            sum1 = tree.tile([P, J * D], F32)
+            nc.vector.tensor_tensor(out=sum1[:], in0=sum2[:, 0, :], in1=sum2[:, 1, :], op=ALU.add)
+            mix = q_pool.tile([P, J * D], F32)
+            nc.vector.scalar_tensor_tensor(
+                out=mix[:], in0=max1[:], scalar=MAX_WEIGHT / MEAN_WEIGHT, in1=sum1[:], op0=ALU.mult, op1=ALU.add
+            )
+
+            for j in range(J):
+                col = u * J + j
+                nc.scalar.activation(
+                    out=x[:, j, D:K], in_=mix[:, j * D : (j + 1) * D], func=ACT.Copy, scale=gate[:, col : col + 1]
+                )
+
+            x_words = x[:].bitcast(F32)
+            xT_ps = psum.tile([P, WORDS, UNIT], F32, tag="xT_ps")
+            for j in range(J):
+                for w in range(WORDS):
+                    nc.tensor.transpose(
+                        out=xT_ps[:, w, j * P : (j + 1) * P], in_=x_words[:, j, w : K // 2 : WORDS], identity=ident_f[:]
+                    )
+            grouped = work.tile([P, UNIT * PACK], BF16, align_bytes=64)
+            nc.scalar.copy(
+                out=grouped[:].bitcast(F32).rearrange("p (r w) -> p r w", w=WORDS),
+                in_=xT_ps[:].rearrange("p w r -> p r w"),
+            )
+            x_codes = work.tile([P, UNIT], U32, align_bytes=64)
+            x_plane = work.tile([P, UNIT], U8, align_bytes=64)
+            nc.vector.quantize_mx(out=x_codes[:].bitcast(FP8X4), scales=x_plane[:], in_=grouped[:])
+
+            yT_ps = psum.tile([P, HALVES, UNIT], F32, tag="yT_ps")
+            yT = work.tile([P, HALVES, UNIT], F32)
+            for h in range(HALVES):
+                nc.tensor.matmul_mx(
+                    out=yT_ps[:, h, :],
+                    lhsT=wf_sb[:, h * 2 * P : (h + 1) * 2 * P].bitcast(FP4X4),
+                    lhsT_scale=wf_plane[:, h * P : (h + 1) * P],
+                    rhs=x_codes[:].bitcast(FP8X4),
+                    rhs_scale=x_plane[:],
+                    start=True,
+                    stop=True,
+                )
+            for h in range(HALVES):
+                nc.scalar.activation(
+                    out=yT[:, h, :], in_=yT_ps[:, h, :], func=ACT.Identity, bias=vec_cols[:, BIAS_F + h : BIAS_F + h + 1]
+                )
+
+            y_ps = psum.tile([P, J, D], F32, tag="y_ps", bufs=2)
+            for j in range(J):
+                for h in range(HALVES):
+                    nc.tensor.transpose(
+                        out=y_ps[:, j, h * P : (h + 1) * P], in_=yT[:, h, j * P : (j + 1) * P], identity=ident_f[:]
+                    )
+            neg_mean = stats.tile([P, J], F32)
+            sq_sum = stats.tile([P, J], F32)
+            for j in range(J):
+                unused_a = work.tile([P, D], BF16, tag="unused")
+                nc.scalar.activation(
+                    out=unused_a[:], in_=y_ps[:, j, :], func=ACT.Identity, scale=-1.0 / D, accum_out=neg_mean[:, j : j + 1]
+                )
+            for j in range(J):
+                unused_b = work.tile([P, D], BF16, tag="unused")
+                nc.scalar.activation(
+                    out=unused_b[:],
+                    in_=y_ps[:, j, :],
+                    func=ACT.Square,
+                    bias=neg_mean[:, j : j + 1],
+                    accum_out=sq_sum[:, j : j + 1],
+                )
+            var_eps = stats.tile([P, J], F32)
+            nc.gpsimd.tensor_scalar(out=var_eps[:], in0=sq_sum[:], scalar1=1.0 / D, scalar2=LN_EPS, op0=ALU.mult, op1=ALU.add)
+            rstd = stats.tile([P, J], F32)
+            nc.gpsimd.tensor_tensor(out=rstd[:], in0=var_eps[:], in1=minus_half[:], op=ALU.pow)
+            shift = stats.tile([P, J], F32)
+            nc.gpsimd.tensor_tensor(out=shift[:], in0=neg_mean[:], in1=rstd[:], op=ALU.mult)
+            z = work.tile([P, J, D], F32)
+            for j in range(J):
+                nc.scalar.activation(
+                    out=z[:, j, :], in_=y_ps[:, j, :], func=ACT.Identity, scale=rstd[:, j : j + 1], bias=shift[:, j : j + 1]
+                )
+
+            zT_ps = psum.tile([P, HALVES, UNIT], F32, tag="zT_ps", bufs=2)
+            for h in range(HALVES):
+                for j in range(J):
+                    nc.tensor.transpose(
+                        out=zT_ps[:, h, j * P : (j + 1) * P], in_=z[:, j, h * P : (h + 1) * P], identity=ident_f[:]
+                    )
+            geluT = work.tile([P, HALVES, UNIT], F32)
+            for h in range(HALVES):
+                nc.scalar.activation(
+                    out=geluT[:, h, :],
+                    in_=zT_ps[:, h, :],
+                    func=ACT.Gelu,
+                    scale=vec_cols[:, LN_G + h : LN_G + h + 1],
+                    bias=vec_cols[:, LN_B + h : LN_B + h + 1],
+                )
+
+            gelu_ps = psum.tile([P, J, D], F32, tag="gelu_ps", bufs=2)
+            for j in range(J):
+                for h in range(HALVES):
+                    nc.tensor.transpose(
+                        out=gelu_ps[:, j, h * P : (h + 1) * P], in_=geluT[:, h, j * P : (j + 1) * P], identity=ident_f[:]
+                    )
+            result = work.tile([P, J, D], F32)
+            for j in range(J):
+                col = u * J + j
+                nc.vector.scalar_tensor_tensor(
+                    out=result[:, j, :],
+                    in0=gelu_ps[:, j, :],
+                    scalar=af_factor[:, col : col + 1],
+                    in1=x[:, j, 0:D],
+                    op0=ALU.mult,
+                    op1=ALU.add,
+                )
+            nc.sync.dma_start(out=out_units[u], in_=result[:].rearrange("p j d -> p (j d)"))

@@ -29,6 +29,10 @@ MAX_WEIGHT = 0.3
 LN_EPS = 1e-5
 
 PREFETCH = 3
+LAST_LAG = 3
+CHUNK = 2
+CHUNKS = UNITS // CHUNK
+CHUNKS_PER_STEP = -(-CHUNKS // LAST_LAG)
 
 FLOPS = 2 * B * L * K * D + 2 * B * L * H * D
 
@@ -42,16 +46,15 @@ def tile_rarevariantawarefusion_pa_t_kernel(
     out_units = out.flatten_outer_dims().rearrange("(u p j) d -> u p (j d)", p=P, j=J)
 
     with ExitStack() as ctx:
+        ctx.enter_context(tc.manual_schedule())
         const = ctx.enter_context(tc.tile_pool(name="const", bufs=1))
         rag_pool = ctx.enter_context(tc.tile_pool(name="rag", bufs=PREFETCH + 1))
-        x_pool = ctx.enter_context(tc.tile_pool(name="x", bufs=PREFETCH + 4))
-        tree = ctx.enter_context(tc.tile_pool(name="tree", bufs=2))
-        q_pool = ctx.enter_context(tc.tile_pool(name="q", bufs=5))
-        work = ctx.enter_context(tc.tile_pool(name="work", bufs=3))
-        stats = ctx.enter_context(tc.tile_pool(name="stats", bufs=4))
+        x_pool = ctx.enter_context(tc.tile_pool(name="x", bufs=PREFETCH + LAST_LAG + 1))
+        work = ctx.enter_context(tc.tile_pool(name="work", bufs=2))
+        stats = ctx.enter_context(tc.tile_pool(name="stats", bufs=3))
+        psum = ctx.enter_context(tc.psum_pool(name="psum", bufs=1))
 
-        rag_of = {}
-        x_of = {}
+        kept = {}
 
         def load_unit(u):
             b, first = u // UNITS_PER_BATCH, (u % UNITS_PER_BATCH) * UNIT
@@ -61,20 +64,10 @@ def tile_rarevariantawarefusion_pa_t_kernel(
             )
             x = x_pool.tile([P, J, K], BF16)
             nc.sync.dma_start(out=x[:, :, 0:D], in_=orig_units[u])
-            rag_of[u] = rag
-            x_of[u] = x
+            kept["rag", u] = rag
+            kept["x", u] = x
 
         load_unit(0)
-
-        ident_f = const.tile([P, P], F32)
-        make_identity(nc, ident_f[:])
-        ident_b = const.tile([P, P], BF16)
-        make_identity(nc, ident_b[:])
-
-        h_all = const.tile([P, UNITS, J * H], BF16)
-        nc.sync.dma_start(out=h_all[:], in_=h_af.flatten_outer_dims().rearrange("(u p j) h -> p u (j h)", p=P, j=J))
-        w2_sb = const.tile([H, D], BF16)
-        nc.sync.dma_start(out=w2_sb[:], in_=w2)
 
         vec_rows = const.tile([P, P], BF16)
         nc.gpsimd.memset(vec_rows[:], 0.0)
@@ -83,6 +76,13 @@ def tile_rarevariantawarefusion_pa_t_kernel(
             nc.sync.dma_start(
                 out=vec_rows[first_row : first_row + HALVES, :], in_=vec.rearrange("(h n) -> h n", h=HALVES)
             )
+        w2_sb = const.tile([H, D], BF16)
+        nc.sync.dma_start(out=w2_sb[:], in_=w2)
+        h_all = const.tile([P, UNITS, J * H], BF16)
+        h_units = h_af.flatten_outer_dims().rearrange("(u p j) h -> p u (j h)", p=P, j=J)
+        for c in range(CHUNKS):
+            nc.sync.dma_start(out=h_all[:, c * CHUNK : (c + 1) * CHUNK, :], in_=h_units[:, c * CHUNK : (c + 1) * CHUNK, :])
+        load_unit(1)
 
         wf_sb = const.tile([P, 2 * D], U8, align_bytes=64)
         nc.sync.dma_start(out=wf_sb[:].bitcast(I32), in_=wf_words[0].bitcast(I32))
@@ -93,100 +93,112 @@ def tile_rarevariantawarefusion_pa_t_kernel(
                 out=wf_plane[32 * quad : 32 * quad + 4, :].bitcast(I32),
                 in_=wf_scales[0, 4 * quad : 4 * quad + 4, :].bitcast(I32),
             )
+        af_sb = const.tile([P, UNITS * J], BF16)
+        nc.sync.dma_start(
+            out=af_sb[:].rearrange("p (u j) -> p u j", j=J),
+            in_=af.rearrange("b l -> (b l)").rearrange("(u p j) -> p u j", p=P, j=J),
+        )
+        load_unit(2)
 
-        af_sb = const.tile([P, UNITS, J], BF16)
-        nc.sync.dma_start(out=af_sb[:], in_=af.rearrange("b l -> (b l)").rearrange("(u p j) -> p u j", p=P, j=J))
-
-        for u in range(1, PREFETCH):
-            load_unit(u)
+        ident_b = const.tile([P, P], BF16)
+        make_identity(nc, ident_b[:])
+        ident_f = const.tile([P, P], F32)
+        make_identity(nc, ident_f[:])
 
         half = const.tile([P, UNITS * J], F32)
         nc.gpsimd.memset(half[:], 0.5)
         minus_half = const.tile([P, J], F32)
         nc.gpsimd.memset(minus_half[:], -0.5)
-        af_flat = af_sb[:].rearrange("p u j -> p (u j)")
         one_minus_af = const.tile([P, UNITS * J], F32)
-        nc.gpsimd.tensor_scalar(out=one_minus_af[:], in0=af_flat, scalar1=-1.0, scalar2=1.0, op0=ALU.mult, op1=ALU.add)
+        nc.gpsimd.tensor_scalar(out=one_minus_af[:], in0=af_sb[:], scalar1=-1.0, scalar2=1.0, op0=ALU.mult, op1=ALU.add)
         af_product = const.tile([P, UNITS * J], F32)
-        nc.gpsimd.tensor_tensor(out=af_product[:], in0=one_minus_af[:], in1=af_flat, op=ALU.mult)
+        nc.gpsimd.tensor_tensor(out=af_product[:], in0=one_minus_af[:], in1=af_sb[:], op=ALU.mult)
         af_factor = const.tile([P, UNITS * J], F32)
         nc.gpsimd.tensor_tensor(out=af_factor[:], in0=af_product[:], in1=half[:], op=ALU.pow)
 
         vec_cols = const.tile([P, 4 * HALVES], F32)
+        vec_ps = psum.tile([P, CHUNK * UNIT], BF16, tag="hT_ps")
+        nc.tensor.transpose(out=vec_ps[:, 0:P], in_=vec_rows[:], identity=ident_b[:])
+        nc.scalar.copy(out=vec_cols[:], in_=vec_ps[:, 0 : 4 * HALVES])
+        b2_cols = const.tile([P, HALVES, P], F32)
+        for h in range(HALVES):
+            nc.scalar.activation(
+                out=b2_cols[:, h, :], in_=ident_f[:], func=ACT.Identity, scale=0.0, bias=vec_cols[:, B2 + h : B2 + h + 1]
+            )
         gate = const.tile([P, UNITS * J], F32)
-        CHUNK = 2
-        with tc.psum_pool(name="gate_psum", bufs=2) as gate_psum, tc.tile_pool(name="gate_sbuf", bufs=2) as gate_sbuf:
-            vec_ps = gate_psum.tile([P, CHUNK * UNIT], BF16, tag="hT_ps")
-            nc.tensor.transpose(out=vec_ps[:, 0:P], in_=vec_rows[:], identity=ident_b[:])
-            nc.scalar.copy(out=vec_cols[:], in_=vec_ps[:, 0 : 4 * HALVES])
+        gate_mean = const.tile([P, UNITS * J], F32)
 
-            for c in range(UNITS // CHUNK):
-                hT_ps = gate_psum.tile([P, CHUNK * UNIT], BF16, tag="hT_ps")
-                for blk in range(CHUNK * J):
-                    u, j = CHUNK * c + blk // J, blk % J
-                    nc.tensor.transpose(
-                        out=hT_ps[:, blk * P : (blk + 1) * P], in_=h_all[:, u, j * H : (j + 1) * H], identity=ident_b[:]
-                    )
-                hT = gate_sbuf.tile([P, CHUNK * UNIT], BF16)
-                nc.scalar.copy(out=hT[:], in_=hT_ps[:])
-                sigT = gate_sbuf.tile([P, HALVES, CHUNK * UNIT], F32)
-                for h in range(HALVES):
-                    logits = gate_psum.tile([P, CHUNK * UNIT], F32, tag="logits")
-                    nc.tensor.matmul(out=logits[:], lhsT=w2_sb[:, h * P : (h + 1) * P], rhs=hT[:], start=True, stop=True)
-                    nc.scalar.activation(
-                        out=sigT[:, h, :], in_=logits[:], func=ACT.Sigmoid, bias=vec_cols[:, B2 + h : B2 + h + 1]
-                    )
-                for uu in range(CHUNK):
-                    sig_ps = gate_psum.tile([P, J, D], F32, tag="sig_ps")
-                    for j in range(J):
-                        blk = uu * J + j
-                        for h in range(HALVES):
-                            nc.tensor.transpose(
-                                out=sig_ps[:, j, h * P : (h + 1) * P],
-                                in_=sigT[:, h, blk * P : (blk + 1) * P],
-                                identity=ident_f[:],
-                            )
-                    for j in range(J):
-                        col = (CHUNK * c + uu) * J + j
-                        unused = gate_sbuf.tile([P, D], BF16, tag="unused")
-                        nc.scalar.activation(
-                            out=unused[:],
-                            in_=sig_ps[:, j, :],
-                            func=ACT.Identity,
-                            scale=MEAN_WEIGHT,
-                            accum_out=gate[:, col : col + 1],
+        def h_to_columns(c):
+            hT_ps = psum.tile([P, CHUNK * UNIT], BF16, tag="hT_ps")
+            for blk in range(CHUNK * J):
+                nc.tensor.transpose(
+                    out=hT_ps[:, blk * P : (blk + 1) * P],
+                    in_=h_all[:, CHUNK * c + blk // J, (blk % J) * H : (blk % J + 1) * H],
+                    identity=ident_b[:],
+                )
+            hT = work.tile([P, CHUNK * UNIT], BF16)
+            nc.scalar.copy(out=hT[:], in_=hT_ps[:])
+            kept["hT", c] = hT
+
+        def gate_chunk(c):
+            hT = kept["hT", c]
+            for uu in range(CHUNK):
+                logits = psum.tile([P, J, D], F32, tag="logits", bufs=2)
+                for j in range(J):
+                    blk = uu * J + j
+                    for h in range(HALVES):
+                        nc.tensor.matmul(
+                            out=logits[:, j, h * P : (h + 1) * P],
+                            lhsT=b2_cols[:, h, :],
+                            rhs=ident_f[:],
+                            is_transpose=True,
+                            start=(h == 0),
+                            stop=False,
                         )
+                    nc.tensor.matmul(
+                        out=logits[:, j, :], lhsT=hT[:, blk * P : (blk + 1) * P], rhs=w2_sb[:], start=False, stop=True
+                    )
+                for j in range(J):
+                    col = (CHUNK * c + uu) * J + j
+                    sigmoids = work.tile([P, D], BF16, tag="unused")
+                    nc.scalar.activation(
+                        out=sigmoids[:], in_=logits[:, j, :], func=ACT.Sigmoid, accum_out=gate[:, col : col + 1]
+                    )
+            cols = slice(c * CHUNK * J, (c + 1) * CHUNK * J)
+            nc.scalar.activation(out=gate_mean[:, cols], in_=gate[:, cols], func=ACT.Copy, scale=MEAN_WEIGHT)
 
-        psum = ctx.enter_context(tc.psum_pool(name="psum", bufs=1))
-
-        for u in range(UNITS):
-            if u + PREFETCH < UNITS:
-                load_unit(u + PREFETCH)
-            rag, x = rag_of[u], x_of[u]
-
-            max4 = tree.tile([P, 4, J * D], BF16)
+        def pool_wide(u):
+            rag = kept["rag", u]
+            max4 = work.tile([P, 4, J * D], BF16)
             nc.vector.tensor_tensor(out=max4[:], in0=rag[:, 0:4, :], in1=rag[:, 4:8, :], op=ALU.max)
-            sum4 = tree.tile([P, 4, J * D], F32)
+            sum4 = work.tile([P, 4, J * D], F32)
             nc.vector.tensor_tensor(out=sum4[:], in0=rag[:, 0:4, :], in1=rag[:, 4:8, :], op=ALU.add)
-            max2 = tree.tile([P, 2, J * D], BF16)
+            max2 = work.tile([P, 2, J * D], BF16)
             nc.vector.tensor_tensor(out=max2[:], in0=max4[:, 0:2, :], in1=max4[:, 2:4, :], op=ALU.max)
-            sum2 = tree.tile([P, 2, J * D], F32)
+            sum2 = work.tile([P, 2, J * D], F32)
             nc.vector.tensor_tensor(out=sum2[:], in0=sum4[:, 0:2, :], in1=sum4[:, 2:4, :], op=ALU.add)
-            max1 = tree.tile([P, J * D], BF16)
+            kept["max2", u] = max2
+            kept["sum2", u] = sum2
+
+        def pool_narrow(u):
+            max2, sum2 = kept["max2", u], kept["sum2", u]
+            max1 = work.tile([P, J * D], BF16)
             nc.vector.tensor_tensor(out=max1[:], in0=max2[:, 0, :], in1=max2[:, 1, :], op=ALU.max)
-            sum1 = tree.tile([P, J * D], F32)
+            sum1 = work.tile([P, J * D], F32)
             nc.vector.tensor_tensor(out=sum1[:], in0=sum2[:, 0, :], in1=sum2[:, 1, :], op=ALU.add)
-            mix = q_pool.tile([P, J * D], F32)
+            mix = work.tile([P, J * D], F32)
             nc.vector.scalar_tensor_tensor(
                 out=mix[:], in0=max1[:], scalar=MAX_WEIGHT / MEAN_WEIGHT, in1=sum1[:], op0=ALU.mult, op1=ALU.add
             )
+            kept["mix", u] = mix
 
+        def x_to_columns(u):
+            x, mix = kept["x", u], kept["mix", u]
             for j in range(J):
                 col = u * J + j
                 nc.scalar.activation(
-                    out=x[:, j, D:K], in_=mix[:, j * D : (j + 1) * D], func=ACT.Copy, scale=gate[:, col : col + 1]
+                    out=x[:, j, D:K], in_=mix[:, j * D : (j + 1) * D], func=ACT.Copy, scale=gate_mean[:, col : col + 1]
                 )
-
             x_words = x[:].bitcast(F32)
             xT_ps = psum.tile([P, WORDS, UNIT], F32, tag="xT_ps")
             for j in range(J):
@@ -194,17 +206,21 @@ def tile_rarevariantawarefusion_pa_t_kernel(
                     nc.tensor.transpose(
                         out=xT_ps[:, w, j * P : (j + 1) * P], in_=x_words[:, j, w : K // 2 : WORDS], identity=ident_f[:]
                     )
+            kept["xT_ps", u] = xT_ps
+
+        def group_words(u):
             grouped = work.tile([P, UNIT * PACK], BF16, align_bytes=64)
             nc.scalar.copy(
                 out=grouped[:].bitcast(F32).rearrange("p (r w) -> p r w", w=WORDS),
-                in_=xT_ps[:].rearrange("p w r -> p r w"),
+                in_=kept["xT_ps", u][:].rearrange("p w r -> p r w"),
             )
+            kept["grouped", u] = grouped
+
+        def quantise_and_multiply(u):
             x_codes = work.tile([P, UNIT], U32, align_bytes=64)
             x_plane = work.tile([P, UNIT], U8, align_bytes=64)
-            nc.vector.quantize_mx(out=x_codes[:].bitcast(FP8X4), scales=x_plane[:], in_=grouped[:])
-
+            nc.vector.quantize_mx(out=x_codes[:].bitcast(FP8X4), scales=x_plane[:], in_=kept["grouped", u][:])
             yT_ps = psum.tile([P, HALVES, UNIT], F32, tag="yT_ps")
-            yT = work.tile([P, HALVES, UNIT], F32)
             for h in range(HALVES):
                 nc.tensor.matmul_mx(
                     out=yT_ps[:, h, :],
@@ -215,76 +231,122 @@ def tile_rarevariantawarefusion_pa_t_kernel(
                     start=True,
                     stop=True,
                 )
+            kept["yT_ps", u] = yT_ps
+
+        def y_to_rows(u):
+            yT = work.tile([P, HALVES, UNIT], F32)
             for h in range(HALVES):
                 nc.scalar.activation(
-                    out=yT[:, h, :], in_=yT_ps[:, h, :], func=ACT.Identity, bias=vec_cols[:, BIAS_F + h : BIAS_F + h + 1]
+                    out=yT[:, h, :],
+                    in_=kept["yT_ps", u][:, h, :],
+                    func=ACT.Identity,
+                    bias=vec_cols[:, BIAS_F + h : BIAS_F + h + 1],
                 )
-
-            y_ps = psum.tile([P, J, D], F32, tag="y_ps", bufs=2)
+            y_ps = psum.tile([P, J, D], F32, tag="y_ps")
             for j in range(J):
                 for h in range(HALVES):
                     nc.tensor.transpose(
                         out=y_ps[:, j, h * P : (h + 1) * P], in_=yT[:, h, j * P : (j + 1) * P], identity=ident_f[:]
                     )
+            kept["y_ps", u] = y_ps
+
+        def statistics(u):
+            y = work.tile([P, J, D], F32)
+            y_sum = stats.tile([P, J], F32)
+            for j in range(J):
+                nc.scalar.activation(
+                    out=y[:, j, :], in_=kept["y_ps", u][:, j, :], func=ACT.Identity, accum_out=y_sum[:, j : j + 1]
+                )
             neg_mean = stats.tile([P, J], F32)
+            nc.scalar.activation(out=neg_mean[:], in_=y_sum[:], func=ACT.Copy, scale=-1.0 / D)
             sq_sum = stats.tile([P, J], F32)
             for j in range(J):
-                unused_a = work.tile([P, D], BF16, tag="unused")
+                squares = work.tile([P, D], BF16, tag="unused")
                 nc.scalar.activation(
-                    out=unused_a[:], in_=y_ps[:, j, :], func=ACT.Identity, scale=-1.0 / D, accum_out=neg_mean[:, j : j + 1]
-                )
-            for j in range(J):
-                unused_b = work.tile([P, D], BF16, tag="unused")
-                nc.scalar.activation(
-                    out=unused_b[:],
-                    in_=y_ps[:, j, :],
+                    out=squares[:],
+                    in_=y[:, j, :],
                     func=ACT.Square,
                     bias=neg_mean[:, j : j + 1],
                     accum_out=sq_sum[:, j : j + 1],
                 )
             var_eps = stats.tile([P, J], F32)
-            nc.gpsimd.tensor_scalar(out=var_eps[:], in0=sq_sum[:], scalar1=1.0 / D, scalar2=LN_EPS, op0=ALU.mult, op1=ALU.add)
+            nc.scalar.activation(out=var_eps[:], in_=sq_sum[:], func=ACT.Copy, scale=1.0 / D, bias=LN_EPS)
             rstd = stats.tile([P, J], F32)
             nc.gpsimd.tensor_tensor(out=rstd[:], in0=var_eps[:], in1=minus_half[:], op=ALU.pow)
+            kept["y", u] = y
+            kept["neg_mean", u] = neg_mean
+            kept["rstd", u] = rstd
+
+        def z_to_columns(u):
+            y, neg_mean, rstd = kept["y", u], kept["neg_mean", u], kept["rstd", u]
             shift = stats.tile([P, J], F32)
-            nc.gpsimd.tensor_tensor(out=shift[:], in0=neg_mean[:], in1=rstd[:], op=ALU.mult)
             z = work.tile([P, J, D], F32)
             for j in range(J):
                 nc.scalar.activation(
-                    out=z[:, j, :], in_=y_ps[:, j, :], func=ACT.Identity, scale=rstd[:, j : j + 1], bias=shift[:, j : j + 1]
+                    out=shift[:, j : j + 1], in_=neg_mean[:, j : j + 1], func=ACT.Copy, scale=rstd[:, j : j + 1]
                 )
-
-            zT_ps = psum.tile([P, HALVES, UNIT], F32, tag="zT_ps", bufs=2)
+            for j in range(J):
+                nc.scalar.activation(
+                    out=z[:, j, :], in_=y[:, j, :], func=ACT.Identity, scale=rstd[:, j : j + 1], bias=shift[:, j : j + 1]
+                )
+            zT_ps = psum.tile([P, HALVES, UNIT], F32, tag="zT_ps")
             for h in range(HALVES):
                 for j in range(J):
                     nc.tensor.transpose(
                         out=zT_ps[:, h, j * P : (j + 1) * P], in_=z[:, j, h * P : (h + 1) * P], identity=ident_f[:]
                     )
+            kept["zT_ps", u] = zT_ps
+
+        def gelu_to_rows(u):
             geluT = work.tile([P, HALVES, UNIT], F32)
             for h in range(HALVES):
                 nc.scalar.activation(
                     out=geluT[:, h, :],
-                    in_=zT_ps[:, h, :],
+                    in_=kept["zT_ps", u][:, h, :],
                     func=ACT.Gelu,
                     scale=vec_cols[:, LN_G + h : LN_G + h + 1],
                     bias=vec_cols[:, LN_B + h : LN_B + h + 1],
                 )
-
-            gelu_ps = psum.tile([P, J, D], F32, tag="gelu_ps", bufs=2)
+            gelu_ps = psum.tile([P, J, D], F32, tag="gelu_ps")
             for j in range(J):
                 for h in range(HALVES):
                     nc.tensor.transpose(
                         out=gelu_ps[:, j, h * P : (h + 1) * P], in_=geluT[:, h, j * P : (j + 1) * P], identity=ident_f[:]
                     )
+            kept["gelu_ps", u] = gelu_ps
+
+        def finish(u):
             result = work.tile([P, J, D], F32)
             for j in range(J):
                 col = u * J + j
                 nc.vector.scalar_tensor_tensor(
                     out=result[:, j, :],
-                    in0=gelu_ps[:, j, :],
+                    in0=kept["gelu_ps", u][:, j, :],
                     scalar=af_factor[:, col : col + 1],
-                    in1=x[:, j, 0:D],
+                    in1=kept["x", u][:, j, 0:D],
                     op0=ALU.mult,
                     op1=ALU.add,
                 )
             nc.sync.dma_start(out=out_units[u], in_=result[:].rearrange("p j d -> p (j d)"))
+
+        def run(stage, u):
+            if 0 <= u < UNITS:
+                stage(u)
+
+        h_to_columns(0)
+        for i in range(UNITS + LAST_LAG):
+            run(load_unit, i + PREFETCH)
+            run(pool_wide, i)
+            run(x_to_columns, i - 1)
+            run(y_to_rows, i - 2)
+            run(z_to_columns, i - LAST_LAG)
+            run(group_words, i - 1)
+            run(statistics, i - 2)
+            run(gelu_to_rows, i - LAST_LAG)
+            run(quantise_and_multiply, i - 1)
+            run(pool_narrow, i)
+            run(finish, i - LAST_LAG)
+            for c in range(i * CHUNKS_PER_STEP, min((i + 1) * CHUNKS_PER_STEP, CHUNKS)):
+                if c + 1 < CHUNKS:
+                    h_to_columns(c + 1)
+                gate_chunk(c)

@@ -67,8 +67,6 @@ def tile_rarevariantawarefusion_pa_t_kernel(
             kept["rag", u] = rag
             kept["x", u] = x
 
-        load_unit(0)
-
         vec_rows = const.tile([P, P], BF16)
         nc.gpsimd.memset(vec_rows[:], 0.0)
         B2, BIAS_F, LN_G, LN_B = 0, 2, 4, 6
@@ -82,6 +80,8 @@ def tile_rarevariantawarefusion_pa_t_kernel(
         h_units = h_af.flatten_outer_dims().rearrange("(u p j) h -> p u (j h)", p=P, j=J)
         for c in range(CHUNKS):
             nc.sync.dma_start(out=h_all[:, c * CHUNK : (c + 1) * CHUNK, :], in_=h_units[:, c * CHUNK : (c + 1) * CHUNK, :])
+            if c == 0:
+                load_unit(0)
         load_unit(1)
 
         wf_sb = const.tile([P, 2 * D], U8, align_bytes=64)
@@ -341,12 +341,12 @@ def tile_rarevariantawarefusion_pa_t_kernel(
             run(y_to_rows, i - 2)
             run(z_to_columns, i - LAST_LAG)
             run(group_words, i - 1)
+            for c in range(i * CHUNKS_PER_STEP, min((i + 1) * CHUNKS_PER_STEP, CHUNKS)):
+                if c + 1 < CHUNKS:
+                    h_to_columns(c + 1)
+                gate_chunk(c)
             run(statistics, i - 2)
             run(gelu_to_rows, i - LAST_LAG)
             run(quantise_and_multiply, i - 1)
             run(pool_narrow, i)
             run(finish, i - LAST_LAG)
-            for c in range(i * CHUNKS_PER_STEP, min((i + 1) * CHUNKS_PER_STEP, CHUNKS)):
-                if c + 1 < CHUNKS:
-                    h_to_columns(c + 1)
-                gate_chunk(c)

@@ -30,6 +30,7 @@ LN_EPS = 1e-5
 
 PREFETCH = 3
 LAST_LAG = 3
+FINISH_LAG = LAST_LAG + 1
 CHUNK = 2
 CHUNKS = UNITS // CHUNK
 CHUNKS_PER_STEP = -(-CHUNKS // LAST_LAG)
@@ -49,7 +50,7 @@ def tile_rarevariantawarefusion_pa_t_kernel(
         ctx.enter_context(tc.manual_schedule())
         const = ctx.enter_context(tc.tile_pool(name="const", bufs=1))
         rag_pool = ctx.enter_context(tc.tile_pool(name="rag", bufs=PREFETCH + 1))
-        x_pool = ctx.enter_context(tc.tile_pool(name="x", bufs=PREFETCH + LAST_LAG + 1))
+        x_pool = ctx.enter_context(tc.tile_pool(name="x", bufs=PREFETCH + FINISH_LAG + 1))
         work = ctx.enter_context(tc.tile_pool(name="work", bufs=2))
         stats = ctx.enter_context(tc.tile_pool(name="stats", bufs=3))
         psum = ctx.enter_context(tc.psum_pool(name="psum", bufs=1))
@@ -67,6 +68,8 @@ def tile_rarevariantawarefusion_pa_t_kernel(
             kept["rag", u] = rag
             kept["x", u] = x
 
+        load_unit(0)
+
         vec_rows = const.tile([P, P], BF16)
         nc.gpsimd.memset(vec_rows[:], 0.0)
         B2, BIAS_F, LN_G, LN_B = 0, 2, 4, 6
@@ -80,8 +83,6 @@ def tile_rarevariantawarefusion_pa_t_kernel(
         h_units = h_af.flatten_outer_dims().rearrange("(u p j) h -> p u (j h)", p=P, j=J)
         for c in range(CHUNKS):
             nc.sync.dma_start(out=h_all[:, c * CHUNK : (c + 1) * CHUNK, :], in_=h_units[:, c * CHUNK : (c + 1) * CHUNK, :])
-            if c == 0:
-                load_unit(0)
         load_unit(1)
 
         wf_sb = const.tile([P, 2 * D], U8, align_bytes=64)
@@ -117,7 +118,7 @@ def tile_rarevariantawarefusion_pa_t_kernel(
         nc.gpsimd.tensor_tensor(out=af_factor[:], in0=af_product[:], in1=half[:], op=ALU.pow)
 
         vec_cols = const.tile([P, 4 * HALVES], F32)
-        vec_ps = psum.tile([P, CHUNK * UNIT], BF16, tag="hT_ps")
+        vec_ps = psum.tile([P, CHUNK * UNIT], BF16, tag="hT_then_gelu", bufs=2)
         nc.tensor.transpose(out=vec_ps[:, 0:P], in_=vec_rows[:], identity=ident_b[:])
         nc.scalar.copy(out=vec_cols[:], in_=vec_ps[:, 0 : 4 * HALVES])
         b2_cols = const.tile([P, HALVES, P], F32)
@@ -129,7 +130,7 @@ def tile_rarevariantawarefusion_pa_t_kernel(
         gate_mean = const.tile([P, UNITS * J], F32)
 
         def h_to_columns(c):
-            hT_ps = psum.tile([P, CHUNK * UNIT], BF16, tag="hT_ps")
+            hT_ps = psum.tile([P, CHUNK * UNIT], BF16, tag="hT_then_gelu", bufs=2)
             for blk in range(CHUNK * J):
                 nc.tensor.transpose(
                     out=hT_ps[:, blk * P : (blk + 1) * P],
@@ -307,7 +308,7 @@ def tile_rarevariantawarefusion_pa_t_kernel(
                     scale=vec_cols[:, LN_G + h : LN_G + h + 1],
                     bias=vec_cols[:, LN_B + h : LN_B + h + 1],
                 )
-            gelu_ps = psum.tile([P, J, D], F32, tag="gelu_ps")
+            gelu_ps = psum.tile([P, J, D], F32, tag="hT_then_gelu", bufs=2)
             for j in range(J):
                 for h in range(HALVES):
                     nc.tensor.transpose(
@@ -334,19 +335,19 @@ def tile_rarevariantawarefusion_pa_t_kernel(
                 stage(u)
 
         h_to_columns(0)
-        for i in range(UNITS + LAST_LAG):
+        for i in range(UNITS + FINISH_LAG):
             run(load_unit, i + PREFETCH)
             run(pool_wide, i)
             run(x_to_columns, i - 1)
             run(y_to_rows, i - 2)
             run(z_to_columns, i - LAST_LAG)
             run(group_words, i - 1)
-            for c in range(i * CHUNKS_PER_STEP, min((i + 1) * CHUNKS_PER_STEP, CHUNKS)):
-                if c + 1 < CHUNKS:
-                    h_to_columns(c + 1)
-                gate_chunk(c)
             run(statistics, i - 2)
             run(gelu_to_rows, i - LAST_LAG)
             run(quantise_and_multiply, i - 1)
             run(pool_narrow, i)
-            run(finish, i - LAST_LAG)
+            run(finish, i - FINISH_LAG)
+            for c in range(i * CHUNKS_PER_STEP, min((i + 1) * CHUNKS_PER_STEP, CHUNKS)):
+                if c + 1 < CHUNKS:
+                    h_to_columns(c + 1)
+                gate_chunk(c)

@@ -31,6 +31,7 @@ LN_EPS = 1e-5
 PREFETCH = 3
 LAST_LAG = 3
 FINISH_LAG = LAST_LAG + 1
+ROW_UNITS = 2
 CHUNK = 2
 CHUNKS = UNITS // CHUNK
 CHUNKS_PER_STEP = -(-CHUNKS // LAST_LAG)
@@ -221,6 +222,20 @@ def tile_rarevariantawarefusion_pa_t_kernel(
             x_codes = work.tile([P, UNIT], U32, align_bytes=64)
             x_plane = work.tile([P, UNIT], U8, align_bytes=64)
             nc.vector.quantize_mx(out=x_codes[:].bitcast(FP8X4), scales=x_plane[:], in_=kept["grouped", u][:])
+            if u >= UNITS - ROW_UNITS:
+                y_rows_ps = psum.tile([P, J, D], F32, tag="yT_ps")
+                for j in range(J):
+                    nc.tensor.matmul_mx(
+                        out=y_rows_ps[:, j, :],
+                        lhsT=x_codes[:, j * P : (j + 1) * P].bitcast(FP8X4),
+                        lhsT_scale=x_plane[:, j * P : (j + 1) * P],
+                        rhs=wf_sb[:].bitcast(FP4X4),
+                        rhs_scale=wf_plane[:],
+                        start=True,
+                        stop=True,
+                    )
+                kept["y_rows_ps", u] = y_rows_ps
+                return
             yT_ps = psum.tile([P, HALVES, UNIT], F32, tag="yT_ps")
             for h in range(HALVES):
                 nc.tensor.matmul_mx(
@@ -258,6 +273,12 @@ def tile_rarevariantawarefusion_pa_t_kernel(
                 nc.scalar.activation(
                     out=y[:, j, :], in_=kept["y_ps", u][:, j, :], func=ACT.Identity, accum_out=y_sum[:, j : j + 1]
                 )
+            kept["y", u] = y
+            kept["y_sum", u] = y_sum
+            variance(u)
+
+        def variance(u):
+            y, y_sum = kept["y", u], kept["y_sum", u]
             neg_mean = stats.tile([P, J], F32)
             nc.scalar.activation(out=neg_mean[:], in_=y_sum[:], func=ACT.Copy, scale=-1.0 / D)
             sq_sum = stats.tile([P, J], F32)
@@ -274,7 +295,6 @@ def tile_rarevariantawarefusion_pa_t_kernel(
             nc.scalar.activation(out=var_eps[:], in_=sq_sum[:], func=ACT.Copy, scale=1.0 / D, bias=LN_EPS)
             rstd = stats.tile([P, J], F32)
             nc.gpsimd.tensor_tensor(out=rstd[:], in0=var_eps[:], in1=minus_half[:], op=ALU.pow)
-            kept["y", u] = y
             kept["neg_mean", u] = neg_mean
             kept["rstd", u] = rstd
 
@@ -330,13 +350,65 @@ def tile_rarevariantawarefusion_pa_t_kernel(
                 )
             nc.sync.dma_start(out=out_units[u], in_=result[:].rearrange("p j d -> p (j d)"))
 
+        def load_row_vectors():
+            row_vecs = const.tile([P, 3, D], BF16)
+            for k, vec in enumerate((bias_f, ln_g, ln_b)):
+                nc.sync.dma_start(out=row_vecs[:, k, :], in_=vec.partition_broadcast(P))
+            kept["row_vecs"] = row_vecs
+
+        def add_bias_rows(u):
+            y = work.tile([P, J, D], F32)
+            y_sum = stats.tile([P, J], F32)
+            for j in range(J):
+                nc.vector.scalar_tensor_tensor(
+                    out=y[:, j, :],
+                    in0=kept["y_rows_ps", u][:, j, :],
+                    scalar=1.0,
+                    in1=kept["row_vecs"][:, 0, :],
+                    op0=ALU.mult,
+                    op1=ALU.add,
+                    accum_out=y_sum[:, j : j + 1],
+                )
+            kept["y", u] = y
+            kept["y_sum", u] = y_sum
+
+        def normalise_rows(u):
+            y, neg_mean, rstd, row_vecs = kept["y", u], kept["neg_mean", u], kept["rstd", u], kept["row_vecs"]
+            shift = stats.tile([P, J], F32)
+            nc.vector.tensor_tensor(out=shift[:], in0=neg_mean[:], in1=rstd[:], op=ALU.mult)
+            z = work.tile([P, J, D], F32)
+            gained = work.tile([P, J, D], F32)
+            yn = work.tile([P, J, D], F32)
+            for j in range(J):
+                nc.vector.tensor_scalar(
+                    out=z[:, j, :],
+                    in0=y[:, j, :],
+                    scalar1=rstd[:, j : j + 1],
+                    scalar2=shift[:, j : j + 1],
+                    op0=ALU.mult,
+                    op1=ALU.add,
+                )
+            for j in range(J):
+                nc.vector.tensor_tensor(out=gained[:, j, :], in0=z[:, j, :], in1=row_vecs[:, 1, :], op=ALU.mult)
+            for j in range(J):
+                nc.vector.tensor_tensor(out=yn[:, j, :], in0=gained[:, j, :], in1=row_vecs[:, 2, :], op=ALU.add)
+            kept["yn", u] = yn
+
+        def gelu_rows(u):
+            gelu_sb = work.tile([P, J, D], F32)
+            for j in range(J):
+                nc.scalar.activation(out=gelu_sb[:, j, :], in_=kept["yn", u][:, j, :], func=ACT.Gelu)
+            kept["gelu_ps", u] = gelu_sb
+
         def run(stage, u):
             if 0 <= u < UNITS:
                 stage(u)
 
         h_to_columns(0)
-        for i in range(UNITS + FINISH_LAG):
+        for i in range(UNITS):
             run(load_unit, i + PREFETCH)
+            if i == UNITS // 2:
+                load_row_vectors()
             run(pool_wide, i)
             run(x_to_columns, i - 1)
             run(y_to_rows, i - 2)
@@ -351,3 +423,22 @@ def tile_rarevariantawarefusion_pa_t_kernel(
                 if c + 1 < CHUNKS:
                     h_to_columns(c + 1)
                 gate_chunk(c)
+
+        assert UNITS == 16 and ROW_UNITS == 2 and LAST_LAG == 3
+        x_to_columns(15)
+        add_bias_rows(14)
+        z_to_columns(13)
+        variance(14)
+        finish(12)
+        group_words(15)
+        quantise_and_multiply(15)
+        gelu_to_rows(13)
+        add_bias_rows(15)
+        normalise_rows(14)
+        variance(15)
+        gelu_rows(14)
+        finish(13)
+        normalise_rows(15)
+        finish(14)
+        gelu_rows(15)
+        finish(15)

@@ -34,9 +34,15 @@ FINISH_LAG = LAST_LAG + 1
 ROW_UNITS = 2
 CHUNK = 2
 CHUNKS = UNITS // CHUNK
-CHUNKS_PER_STEP = -(-CHUNKS // LAST_LAG)
+CHUNK_PLAN = (2, 2, 1, 1, 1, 1)
+FIRST_GELU = len(CHUNK_PLAN)
+WAITING = FIRST_GELU - LAST_LAG + 1
 
 FLOPS = 2 * B * L * K * D + 2 * B * L * H * D
+
+
+def norm_step(u):
+    return max(u + LAST_LAG, FIRST_GELU + u // 2)
 
 
 def tile_rarevariantawarefusion_pa_t_kernel(
@@ -51,9 +57,9 @@ def tile_rarevariantawarefusion_pa_t_kernel(
         ctx.enter_context(tc.manual_schedule())
         const = ctx.enter_context(tc.tile_pool(name="const", bufs=1))
         rag_pool = ctx.enter_context(tc.tile_pool(name="rag", bufs=PREFETCH + 1))
-        x_pool = ctx.enter_context(tc.tile_pool(name="x", bufs=PREFETCH + FINISH_LAG + 1))
+        x_pool = ctx.enter_context(tc.tile_pool(name="x", bufs=PREFETCH + FINISH_LAG + WAITING + 1))
         work = ctx.enter_context(tc.tile_pool(name="work", bufs=2))
-        stats = ctx.enter_context(tc.tile_pool(name="stats", bufs=3))
+        stats = ctx.enter_context(tc.tile_pool(name="stats", bufs=3 + WAITING))
         psum = ctx.enter_context(tc.psum_pool(name="psum", bufs=1))
 
         kept = {}
@@ -267,7 +273,7 @@ def tile_rarevariantawarefusion_pa_t_kernel(
             kept["y_ps", u] = y_ps
 
         def statistics(u):
-            y = work.tile([P, J, D], F32)
+            y = work.tile([P, J, D], F32, bufs=2 + WAITING)
             y_sum = stats.tile([P, J], F32)
             for j in range(J):
                 nc.scalar.activation(
@@ -281,6 +287,11 @@ def tile_rarevariantawarefusion_pa_t_kernel(
             y, y_sum = kept["y", u], kept["y_sum", u]
             neg_mean = stats.tile([P, J], F32)
             nc.scalar.activation(out=neg_mean[:], in_=y_sum[:], func=ACT.Copy, scale=-1.0 / D)
+            kept["neg_mean", u] = neg_mean
+            squares_and_rstd(u)
+
+        def squares_and_rstd(u):
+            y, neg_mean = kept["y", u], kept["neg_mean", u]
             sq_sum = stats.tile([P, J], F32)
             for j in range(J):
                 squares = work.tile([P, D], BF16, tag="unused")
@@ -295,10 +306,13 @@ def tile_rarevariantawarefusion_pa_t_kernel(
             nc.scalar.activation(out=var_eps[:], in_=sq_sum[:], func=ACT.Copy, scale=1.0 / D, bias=LN_EPS)
             rstd = stats.tile([P, J], F32)
             nc.gpsimd.tensor_tensor(out=rstd[:], in0=var_eps[:], in1=minus_half[:], op=ALU.pow)
-            kept["neg_mean", u] = neg_mean
             kept["rstd", u] = rstd
 
         def z_to_columns(u):
+            z_rows(u)
+            z_transposes(u)
+
+        def z_rows(u):
             y, neg_mean, rstd = kept["y", u], kept["neg_mean", u], kept["rstd", u]
             shift = stats.tile([P, J], F32)
             z = work.tile([P, J, D], F32)
@@ -310,6 +324,10 @@ def tile_rarevariantawarefusion_pa_t_kernel(
                 nc.scalar.activation(
                     out=z[:, j, :], in_=y[:, j, :], func=ACT.Identity, scale=rstd[:, j : j + 1], bias=shift[:, j : j + 1]
                 )
+            kept["z", u] = z
+
+        def z_transposes(u):
+            z = kept["z", u]
             zT_ps = psum.tile([P, HALVES, UNIT], F32, tag="zT_ps")
             for h in range(HALVES):
                 for j in range(J):
@@ -356,42 +374,81 @@ def tile_rarevariantawarefusion_pa_t_kernel(
                 nc.sync.dma_start(out=row_vecs[:, k, :], in_=vec.partition_broadcast(P))
             kept["row_vecs"] = row_vecs
 
-        def add_bias_rows(u):
-            y = work.tile([P, J, D], F32)
-            y_sum = stats.tile([P, J], F32)
+        def group_and_quantise(u, j):
+            if j == 0:
+                grouped = work.tile([P, UNIT * PACK], BF16, align_bytes=64)
+                x_codes = work.tile([P, UNIT], U32, align_bytes=64)
+                x_plane = work.tile([P, UNIT], U8, align_bytes=64)
+                kept["grouped", u], kept["x_codes", u], kept["x_plane", u] = grouped, x_codes, x_plane
+            grouped, x_codes, x_plane = kept["grouped", u], kept["x_codes", u], kept["x_plane", u]
+            nc.scalar.copy(
+                out=grouped[:, j * P * PACK : (j + 1) * P * PACK].bitcast(F32).rearrange("p (r w) -> p r w", w=WORDS),
+                in_=kept["xT_ps", u][:, :, j * P : (j + 1) * P].rearrange("p w r -> p r w"),
+            )
+            nc.vector.quantize_mx(
+                out=x_codes[:, j * P : (j + 1) * P].bitcast(FP8X4),
+                scales=x_plane[:, j * P : (j + 1) * P],
+                in_=grouped[:, j * P * PACK : (j + 1) * P * PACK],
+            )
+
+        def multiply_rows(u, j):
+            if j == 0:
+                y_rows_ps = psum.tile([P, J, D], F32, tag="yT_ps")
+                kept["y_rows_ps", u] = y_rows_ps
+            nc.tensor.matmul_mx(
+                out=kept["y_rows_ps", u][:, j, :],
+                lhsT=kept["x_codes", u][:, j * P : (j + 1) * P].bitcast(FP8X4),
+                lhsT_scale=kept["x_plane", u][:, j * P : (j + 1) * P],
+                rhs=wf_sb[:].bitcast(FP4X4),
+                rhs_scale=wf_plane[:],
+                start=True,
+                stop=True,
+            )
+
+        def add_bias_rows(u, j):
+            if j == 0:
+                y = work.tile([P, J, D], F32, bufs=2 + WAITING)
+                y_sum = stats.tile([P, J], F32)
+                kept["y", u], kept["y_sum", u] = y, y_sum
+            nc.vector.scalar_tensor_tensor(
+                out=kept["y", u][:, j, :],
+                in0=kept["y_rows_ps", u][:, j, :],
+                scalar=1.0,
+                in1=kept["row_vecs"][:, 0, :],
+                op0=ALU.mult,
+                op1=ALU.add,
+                accum_out=kept["y_sum", u][:, j : j + 1],
+            )
+
+        def negate_mean(u):
+            neg_mean = stats.tile([P, J], F32)
+            nc.vector.tensor_scalar_mul(out=neg_mean[:], in0=kept["y_sum", u][:], scalar1=-1.0 / D)
+            kept["neg_mean", u] = neg_mean
+
+        def centre_rows(u):
+            centred = work.tile([P, J, D], F32)
             for j in range(J):
                 nc.vector.scalar_tensor_tensor(
-                    out=y[:, j, :],
-                    in0=kept["y_rows_ps", u][:, j, :],
-                    scalar=1.0,
-                    in1=kept["row_vecs"][:, 0, :],
-                    op0=ALU.mult,
-                    op1=ALU.add,
-                    accum_out=y_sum[:, j : j + 1],
+                    out=centred[:, j, :],
+                    in0=kept["y", u][:, j, :],
+                    scalar=kept["neg_mean", u][:, j : j + 1],
+                    in1=kept["row_vecs"][:, 1, :],
+                    op0=ALU.add,
+                    op1=ALU.mult,
                 )
-            kept["y", u] = y
-            kept["y_sum", u] = y_sum
+            kept["centred", u] = centred
 
         def normalise_rows(u):
-            y, neg_mean, rstd, row_vecs = kept["y", u], kept["neg_mean", u], kept["rstd", u], kept["row_vecs"]
-            shift = stats.tile([P, J], F32)
-            nc.vector.tensor_tensor(out=shift[:], in0=neg_mean[:], in1=rstd[:], op=ALU.mult)
-            z = work.tile([P, J, D], F32)
-            gained = work.tile([P, J, D], F32)
             yn = work.tile([P, J, D], F32)
             for j in range(J):
-                nc.vector.tensor_scalar(
-                    out=z[:, j, :],
-                    in0=y[:, j, :],
-                    scalar1=rstd[:, j : j + 1],
-                    scalar2=shift[:, j : j + 1],
+                nc.vector.scalar_tensor_tensor(
+                    out=yn[:, j, :],
+                    in0=kept["centred", u][:, j, :],
+                    scalar=kept["rstd", u][:, j : j + 1],
+                    in1=kept["row_vecs"][:, 2, :],
                     op0=ALU.mult,
                     op1=ALU.add,
                 )
-            for j in range(J):
-                nc.vector.tensor_tensor(out=gained[:, j, :], in0=z[:, j, :], in1=row_vecs[:, 1, :], op=ALU.mult)
-            for j in range(J):
-                nc.vector.tensor_tensor(out=yn[:, j, :], in0=gained[:, j, :], in1=row_vecs[:, 2, :], op=ALU.add)
             kept["yn", u] = yn
 
         def gelu_rows(u):
@@ -405,40 +462,64 @@ def tile_rarevariantawarefusion_pa_t_kernel(
                 stage(u)
 
         h_to_columns(0)
+        chunks_done = 0
         for i in range(UNITS):
+            normed = [u for u in range(UNITS - ROW_UNITS) if norm_step(u) == i]
+            before = [u for u in range(UNITS - ROW_UNITS) if norm_step(u) == i - 1]
             run(load_unit, i + PREFETCH)
             if i == UNITS // 2:
                 load_row_vectors()
             run(pool_wide, i)
             run(x_to_columns, i - 1)
             run(y_to_rows, i - 2)
-            run(z_to_columns, i - LAST_LAG)
+            for u in normed[:1]:
+                z_to_columns(u)
             run(group_words, i - 1)
-            run(statistics, i - 2)
-            run(gelu_to_rows, i - LAST_LAG)
-            run(quantise_and_multiply, i - 1)
-            run(pool_narrow, i)
-            run(finish, i - FINISH_LAG)
-            for c in range(i * CHUNKS_PER_STEP, min((i + 1) * CHUNKS_PER_STEP, CHUNKS)):
+            for c in range(chunks_done, chunks_done + (CHUNK_PLAN[i] if i < len(CHUNK_PLAN) else 0)):
                 if c + 1 < CHUNKS:
                     h_to_columns(c + 1)
                 gate_chunk(c)
+                chunks_done = c + 1
+            run(statistics, i - 2)
+            for u in before[:1]:
+                finish(u)
+            for u in normed[:1]:
+                gelu_to_rows(u)
+            for u in normed[1:]:
+                z_to_columns(u)
+            run(quantise_and_multiply, i - 1)
+            for u in before[1:]:
+                finish(u)
+            for u in normed[1:]:
+                gelu_to_rows(u)
+            run(pool_narrow, i)
+        assert chunks_done == CHUNKS
 
-        assert UNITS == 16 and ROW_UNITS == 2 and LAST_LAG == 3
-        x_to_columns(15)
-        add_bias_rows(14)
-        z_to_columns(13)
-        variance(14)
-        finish(12)
-        group_words(15)
-        quantise_and_multiply(15)
-        gelu_to_rows(13)
-        add_bias_rows(15)
-        normalise_rows(14)
-        variance(15)
-        gelu_rows(14)
-        finish(13)
-        normalise_rows(15)
-        finish(14)
-        gelu_rows(15)
-        finish(15)
+        assert ROW_UNITS == 2 and LAST_LAG == 3
+        last = UNITS - 1
+        x_to_columns(last)
+        add_bias_rows(last - 1, 0)
+        add_bias_rows(last - 1, 1)
+        negate_mean(last - 1)
+        z_rows(last - 2)
+        finish(last - 3)
+        group_and_quantise(last, 0)
+        multiply_rows(last, 0)
+        squares_and_rstd(last - 1)
+        centre_rows(last - 1)
+        z_transposes(last - 2)
+        group_and_quantise(last, 1)
+        multiply_rows(last, 1)
+        add_bias_rows(last, 0)
+        gelu_to_rows(last - 2)
+        normalise_rows(last - 1)
+        add_bias_rows(last, 1)
+        negate_mean(last)
+        gelu_rows(last - 1)
+        squares_and_rstd(last)
+        centre_rows(last)
+        finish(last - 1)
+        normalise_rows(last)
+        finish(last - 2)
+        gelu_rows(last)
+        finish(last)

@@ -481,18 +481,21 @@ def tile_rarevariantawarefusion_pa_t_kernel(
                 gate_chunk(c)
                 chunks_done = c + 1
             run(statistics, i - 2)
-            for u in before[:1]:
+            early = before[: max(0, len(before) + len(normed) - 2)]
+            for u in early[:1]:
                 finish(u)
             for u in normed[:1]:
                 gelu_to_rows(u)
             for u in normed[1:]:
                 z_to_columns(u)
             run(quantise_and_multiply, i - 1)
-            for u in before[1:]:
+            for u in early[1:]:
                 finish(u)
             for u in normed[1:]:
                 gelu_to_rows(u)
             run(pool_narrow, i)
+            for u in before[len(early) :]:
+                finish(u)
         assert chunks_done == CHUNKS
 
         assert ROW_UNITS == 2 and LAST_LAG == 3

@@ -32,6 +32,7 @@ PREFETCH = 3
 LAST_LAG = 3
 FINISH_LAG = LAST_LAG + 1
 ROW_UNITS = 2
+EARLY_ROW_UNITS = (0, 2)
 CHUNK = 2
 CHUNKS = UNITS // CHUNK
 CHUNK_PLAN = (2, 2, 1, 1, 1, 1)
@@ -41,8 +42,21 @@ WAITING = FIRST_GELU - LAST_LAG + 1
 FLOPS = 2 * B * L * K * D + 2 * B * L * H * D
 
 
-def norm_step(u):
-    return max(u + LAST_LAG, FIRST_GELU + u // 2)
+def in_rows(u):
+    return u in EARLY_ROW_UNITS or u >= UNITS - ROW_UNITS
+
+
+def norm_steps():
+    steps = {}
+    step, taken = FIRST_GELU, 0
+    for u in range(UNITS):
+        if in_rows(u):
+            continue
+        if u + LAST_LAG > step or taken == 2:
+            step, taken = max(step + 1, u + LAST_LAG), 0
+        steps[u] = step
+        taken += 1
+    return steps
 
 
 def tile_rarevariantawarefusion_pa_t_kernel(
@@ -107,6 +121,10 @@ def tile_rarevariantawarefusion_pa_t_kernel(
             in_=af.rearrange("b l -> (b l)").rearrange("(u p j) -> p u j", p=P, j=J),
         )
         load_unit(2)
+        row_vecs = const.tile([P, 3, D], BF16)
+        for k, vec in enumerate((bias_f, ln_g, ln_b)):
+            nc.sync.dma_start(out=row_vecs[:, k, :], in_=vec.partition_broadcast(P))
+        kept["row_vecs"] = row_vecs
 
         ident_b = const.tile([P, P], BF16)
         make_identity(nc, ident_b[:])
@@ -228,7 +246,7 @@ def tile_rarevariantawarefusion_pa_t_kernel(
             x_codes = work.tile([P, UNIT], U32, align_bytes=64)
             x_plane = work.tile([P, UNIT], U8, align_bytes=64)
             nc.vector.quantize_mx(out=x_codes[:].bitcast(FP8X4), scales=x_plane[:], in_=kept["grouped", u][:])
-            if u >= UNITS - ROW_UNITS:
+            if in_rows(u):
                 y_rows_ps = psum.tile([P, J, D], F32, tag="yT_ps")
                 for j in range(J):
                     nc.tensor.matmul_mx(
@@ -368,12 +386,6 @@ def tile_rarevariantawarefusion_pa_t_kernel(
                 )
             nc.sync.dma_start(out=out_units[u], in_=result[:].rearrange("p j d -> p (j d)"))
 
-        def load_row_vectors():
-            row_vecs = const.tile([P, 3, D], BF16)
-            for k, vec in enumerate((bias_f, ln_g, ln_b)):
-                nc.sync.dma_start(out=row_vecs[:, k, :], in_=vec.partition_broadcast(P))
-            kept["row_vecs"] = row_vecs
-
         def group_and_quantise(u, j):
             if j == 0:
                 grouped = work.tile([P, UNIT * PACK], BF16, align_bytes=64)
@@ -463,15 +475,22 @@ def tile_rarevariantawarefusion_pa_t_kernel(
 
         h_to_columns(0)
         chunks_done = 0
+        norm_step = norm_steps()
         for i in range(UNITS):
-            normed = [u for u in range(UNITS - ROW_UNITS) if norm_step(u) == i]
-            before = [u for u in range(UNITS - ROW_UNITS) if norm_step(u) == i - 1]
+            normed = [u for u in sorted(norm_step) if norm_step[u] == i]
+            before = [u for u in sorted(norm_step) if norm_step[u] == i - 1]
+            rows_now = i - 2 in EARLY_ROW_UNITS
             run(load_unit, i + PREFETCH)
-            if i == UNITS // 2:
-                load_row_vectors()
+            if rows_now:
+                add_bias_rows(i - 2, 0)
+                add_bias_rows(i - 2, 1)
+                negate_mean(i - 2)
             run(pool_wide, i)
             run(x_to_columns, i - 1)
-            run(y_to_rows, i - 2)
+            if rows_now:
+                squares_and_rstd(i - 2)
+            else:
+                run(y_to_rows, i - 2)
             for u in normed[:1]:
                 z_to_columns(u)
             run(group_words, i - 1)
@@ -480,7 +499,10 @@ def tile_rarevariantawarefusion_pa_t_kernel(
                     h_to_columns(c + 1)
                 gate_chunk(c)
                 chunks_done = c + 1
-            run(statistics, i - 2)
+            if rows_now:
+                centre_rows(i - 2)
+            else:
+                run(statistics, i - 2)
             early = before[: max(0, len(before) + len(normed) - 2)]
             for u in early[:1]:
                 finish(u)
@@ -489,6 +511,11 @@ def tile_rarevariantawarefusion_pa_t_kernel(
             for u in normed[1:]:
                 z_to_columns(u)
             run(quantise_and_multiply, i - 1)
+            if i - LAST_LAG in EARLY_ROW_UNITS:
+                normalise_rows(i - LAST_LAG)
+            for u in EARLY_ROW_UNITS:
+                if max(u + LAST_LAG, FIRST_GELU) == i:
+                    gelu_rows(u)
             for u in early[1:]:
                 finish(u)
             for u in normed[1:]:
@@ -496,6 +523,9 @@ def tile_rarevariantawarefusion_pa_t_kernel(
             run(pool_narrow, i)
             for u in before[len(early) :]:
                 finish(u)
+            for u in EARLY_ROW_UNITS:
+                if max(u + LAST_LAG, FIRST_GELU) == i - 1:
+                    finish(u)
         assert chunks_done == CHUNKS
 
         assert ROW_UNITS == 2 and LAST_LAG == 3

@@ -212,6 +212,11 @@ def tile_rarevariantawarefusion_pa_t_kernel(
             nc.vector.tensor_tensor(out=max1[:], in0=max2[:, 0, :], in1=max2[:, 1, :], op=ALU.max)
             sum1 = work.tile([P, J * D], F32)
             nc.vector.tensor_tensor(out=sum1[:], in0=sum2[:, 0, :], in1=sum2[:, 1, :], op=ALU.add)
+            kept["max1", u] = max1
+            kept["sum1", u] = sum1
+
+        def mix_sum_and_max(u):
+            max1, sum1 = kept["max1", u], kept["sum1", u]
             mix = work.tile([P, J * D], F32)
             nc.vector.scalar_tensor_tensor(
                 out=mix[:], in0=max1[:], scalar=MAX_WEIGHT / MEAN_WEIGHT, in1=sum1[:], op0=ALU.mult, op1=ALU.add
@@ -521,8 +526,12 @@ def tile_rarevariantawarefusion_pa_t_kernel(
             for u in normed[1:]:
                 gelu_to_rows(u)
             run(pool_narrow, i)
+            if i == UNITS - 1:
+                mix_sum_and_max(i)
             for u in before[len(early) :]:
                 finish(u)
+            if i < UNITS - 1:
+                mix_sum_and_max(i)
             for u in EARLY_ROW_UNITS:
                 if max(u + LAST_LAG, FIRST_GELU) == i - 1:
                     finish(u)

from contextlib import ExitStack

import concourse.mybir as mybir
from concourse.masks import make_identity

F32 = mybir.dt.float32
BF16 = mybir.dt.bfloat16
I32 = mybir.dt.int32
U32 = mybir.dt.uint32
U8 = mybir.dt.uint8
FP8X4 = mybir.dt.float8_e4m3fn_x4
FP4X4 = mybir.dt.float4_e2m1fn_x4
ACT = mybir.ActivationFunctionType
ALU = mybir.AluOpType

P = 128
B, REFS, L, D, H = 8, 8, 512, 256, 128
J = 2
UNIT = P * J
UNITS = B * L // UNIT
UNITS_PER_BATCH = L // UNIT
HALVES = D // P
PACK = 4
WORDS = 2
K = 2 * D

MEAN_WEIGHT = 0.7 / REFS
MAX_WEIGHT = 0.3
LN_EPS = 1e-5

PREFETCH = 3
LAST_LAG = 3
FINISH_LAG = LAST_LAG + 1
ROW_UNITS = 2
EARLY_ROW_UNITS = (0, 2)
CHUNK = 2
CHUNKS = UNITS // CHUNK
CHUNK_PLAN = (2, 2, 1, 1, 1, 1)
FIRST_GELU = len(CHUNK_PLAN)
WAITING = FIRST_GELU - LAST_LAG + 1

FLOPS = 2 * B * L * K * D + 2 * B * L * H * D


def in_rows(u):
    return u in EARLY_ROW_UNITS or u >= UNITS - ROW_UNITS


def norm_steps():
    steps = {}
    step, taken = FIRST_GELU, 0
    for u in range(UNITS):
        if in_rows(u):
            continue
        if u + LAST_LAG > step or taken == 2:
            step, taken = max(step + 1, u + LAST_LAG), 0
        steps[u] = step
        taken += 1
    return steps


def tile_rarevariantawarefusion_pa_t_kernel(
    tc, orig_feat, rag_feat, af, h_af, w2, b2, wf_words, wf_scales, bias_f, ln_g, ln_b, out
):
    nc = tc.nc

    orig_units = orig_feat.flatten_outer_dims().rearrange("(u p j) d -> u p j d", p=P, j=J)
    out_units = out.flatten_outer_dims().rearrange("(u p j) d -> u p (j d)", p=P, j=J)

    with ExitStack() as ctx:
        ctx.enter_context(tc.manual_schedule())
        const = ctx.enter_context(tc.tile_pool(name="const", bufs=1))
        rag_pool = ctx.enter_context(tc.tile_pool(name="rag", bufs=PREFETCH + 1))
        x_pool = ctx.enter_context(tc.tile_pool(name="x", bufs=PREFETCH + FINISH_LAG + WAITING + 1))
        work = ctx.enter_context(tc.tile_pool(name="work", bufs=2))
        stats = ctx.enter_context(tc.tile_pool(name="stats", bufs=3 + WAITING))
        psum = ctx.enter_context(tc.psum_pool(name="psum", bufs=1))

        kept = {}

        def load_unit(u):
            b, first = u // UNITS_PER_BATCH, (u % UNITS_PER_BATCH) * UNIT
            rag = rag_pool.tile([P, REFS, J * D], BF16)
            nc.sync.dma_start(
                out=rag[:], in_=rag_feat[b, :, first : first + UNIT, :].rearrange("k (p j) d -> p k (j d)", j=J)
            )
            x = x_pool.tile([P, J, K], BF16)
            nc.sync.dma_start(out=x[:, :, 0:D], in_=orig_units[u])
            kept["rag", u] = rag
            kept["x", u] = x

        load_unit(0)

        vec_rows = const.tile([P, P], BF16)
        nc.gpsimd.memset(vec_rows[:], 0.0)
        B2, BIAS_F, LN_G, LN_B = 0, 2, 4, 6
        for first_row, vec in ((B2, b2), (BIAS_F, bias_f), (LN_G, ln_g), (LN_B, ln_b)):
            nc.sync.dma_start(
                out=vec_rows[first_row : first_row + HALVES, :], in_=vec.rearrange("(h n) -> h n", h=HALVES)
            )
        w2_sb = const.tile([H, D], BF16)
        nc.sync.dma_start(out=w2_sb[:], in_=w2)
        h_all = const.tile([P, UNITS, J * H], BF16)
        h_units = h_af.flatten_outer_dims().rearrange("(u p j) h -> p u (j h)", p=P, j=J)
        for c in range(CHUNKS):
            nc.sync.dma_start(out=h_all[:, c * CHUNK : (c + 1) * CHUNK, :], in_=h_units[:, c * CHUNK : (c + 1) * CHUNK, :])
        load_unit(1)

        wf_sb = const.tile([P, 2 * D], U8, align_bytes=64)
        nc.sync.dma_start(out=wf_sb[:].bitcast(I32), in_=wf_words[0].bitcast(I32))
        wf_plane = const.tile([P, D], U8, align_bytes=64)
        nc.vector.memset(wf_plane[:].bitcast(I32), 0)
        for quad in range(4):
            nc.sync.dma_start(
                out=wf_plane[32 * quad : 32 * quad + 4, :].bitcast(I32),
                in_=wf_scales[0, 4 * quad : 4 * quad + 4, :].bitcast(I32),
            )
        af_sb = const.tile([P, UNITS * J], BF16)
        nc.sync.dma_start(
            out=af_sb[:].rearrange("p (u j) -> p u j", j=J),
            in_=af.rearrange("b l -> (b l)").rearrange("(u p j) -> p u j", p=P, j=J),
        )
        load_unit(2)
        row_vecs = const.tile([P, 3, D], BF16)
        for k, vec in enumerate((bias_f, ln_g, ln_b)):
            nc.sync.dma_start(out=row_vecs[:, k, :], in_=vec.partition_broadcast(P))
        kept["row_vecs"] = row_vecs

        ident_b = const.tile([P, P], BF16)
        make_identity(nc, ident_b[:])
        ident_f = const.tile([P, P], F32)
        make_identity(nc, ident_f[:])

        half = const.tile([P, UNITS * J], F32)
        nc.gpsimd.memset(half[:], 0.5)
        minus_half = const.tile([P, J], F32)
        nc.gpsimd.memset(minus_half[:], -0.5)
        one_minus_af = const.tile([P, UNITS * J], F32)
        nc.gpsimd.tensor_scalar(out=one_minus_af[:], in0=af_sb[:], scalar1=-1.0, scalar2=1.0, op0=ALU.mult, op1=ALU.add)
        af_product = const.tile([P, UNITS * J], F32)
        nc.gpsimd.tensor_tensor(out=af_product[:], in0=one_minus_af[:], in1=af_sb[:], op=ALU.mult)
        af_factor = const.tile([P, UNITS * J], F32)
        nc.gpsimd.tensor_tensor(out=af_factor[:], in0=af_product[:], in1=half[:], op=ALU.pow)

        vec_cols = const.tile([P, 4 * HALVES], F32)
        vec_ps = psum.tile([P, CHUNK * UNIT], BF16, tag="hT_then_gelu", bufs=2)
        nc.tensor.transpose(out=vec_ps[:, 0:P], in_=vec_rows[:], identity=ident_b[:])
        nc.scalar.copy(out=vec_cols[:], in_=vec_ps[:, 0 : 4 * HALVES])
        b2_cols = const.tile([P, HALVES, P], F32)
        for h in range(HALVES):
            nc.scalar.activation(
                out=b2_cols[:, h, :], in_=ident_f[:], func=ACT.Identity, scale=0.0, bias=vec_cols[:, B2 + h : B2 + h + 1]
            )
        gate = const.tile([P, UNITS * J], F32)
        gate_mean = const.tile([P, UNITS * J], F32)

        def h_to_columns(c):
            hT_ps = psum.tile([P, CHUNK * UNIT], BF16, tag="hT_then_gelu", bufs=2)
            for blk in range(CHUNK * J):
                nc.tensor.transpose(
                    out=hT_ps[:, blk * P : (blk + 1) * P],
                    in_=h_all[:, CHUNK * c + blk // J, (blk % J) * H : (blk % J + 1) * H],
                    identity=ident_b[:],
                )
            hT = work.tile([P, CHUNK * UNIT], BF16)
            nc.scalar.copy(out=hT[:], in_=hT_ps[:])
            kept["hT", c] = hT

        def gate_chunk(c):
            hT = kept["hT", c]
            for uu in range(CHUNK):
                logits = psum.tile([P, J, D], F32, tag="logits", bufs=2)
                for j in range(J):
                    blk = uu * J + j
                    for h in range(HALVES):
                        nc.tensor.matmul(
                            out=logits[:, j, h * P : (h + 1) * P],
                            lhsT=b2_cols[:, h, :],
                            rhs=ident_f[:],
                            is_transpose=True,
                            start=(h == 0),
                            stop=False,
                        )
                    nc.tensor.matmul(
                        out=logits[:, j, :], lhsT=hT[:, blk * P : (blk + 1) * P], rhs=w2_sb[:], start=False, stop=True
                    )
                for j in range(J):
                    col = (CHUNK * c + uu) * J + j
                    sigmoids = work.tile([P, D], BF16, tag="unused")
                    nc.scalar.activation(
                        out=sigmoids[:], in_=logits[:, j, :], func=ACT.Sigmoid, accum_out=gate[:, col : col + 1]
                    )
            cols = slice(c * CHUNK * J, (c + 1) * CHUNK * J)
            nc.scalar.activation(out=gate_mean[:, cols], in_=gate[:, cols], func=ACT.Copy, scale=MEAN_WEIGHT)

        def pool_wide(u):
            rag = kept["rag", u]
            max4 = work.tile([P, 4, J * D], BF16)
            nc.vector.tensor_tensor(out=max4[:], in0=rag[:, 0:4, :], in1=rag[:, 4:8, :], op=ALU.max)
            sum4 = work.tile([P, 4, J * D], F32)
            nc.vector.tensor_tensor(out=sum4[:], in0=rag[:, 0:4, :], in1=rag[:, 4:8, :], op=ALU.add)
            max2 = work.tile([P, 2, J * D], BF16)
            nc.vector.tensor_tensor(out=max2[:], in0=max4[:, 0:2, :], in1=max4[:, 2:4, :], op=ALU.max)
            sum2 = work.tile([P, 2, J * D], F32)
            nc.vector.tensor_tensor(out=sum2[:], in0=sum4[:, 0:2, :], in1=sum4[:, 2:4, :], op=ALU.add)
            kept["max2", u] = max2
            kept["sum2", u] = sum2

        def pool_narrow(u):
            max2, sum2 = kept["max2", u], kept["sum2", u]
            max1 = work.tile([P, J * D], BF16)
            nc.vector.tensor_tensor(out=max1[:], in0=max2[:, 0, :], in1=max2[:, 1, :], op=ALU.max)
            sum1 = work.tile([P, J * D], F32)
            nc.vector.tensor_tensor(out=sum1[:], in0=sum2[:, 0, :], in1=sum2[:, 1, :], op=ALU.add)
            kept["max1", u] = max1
            kept["sum1", u] = sum1

        def mix_sum_and_max(u):
            max1, sum1 = kept["max1", u], kept["sum1", u]
            mix = work.tile([P, J * D], F32)
            nc.vector.scalar_tensor_tensor(
                out=mix[:], in0=max1[:], scalar=MAX_WEIGHT / MEAN_WEIGHT, in1=sum1[:], op0=ALU.mult, op1=ALU.add
            )
            kept["mix", u] = mix

        def x_to_columns(u):
            x, mix = kept["x", u], kept["mix", u]
            for j in range(J):
                col = u * J + j
                nc.scalar.activation(
                    out=x[:, j, D:K], in_=mix[:, j * D : (j + 1) * D], func=ACT.Copy, scale=gate_mean[:, col : col + 1]
                )
            x_words = x[:].bitcast(F32)
            xT_ps = psum.tile([P, WORDS, UNIT], F32, tag="xT_ps")
            for j in range(J):
                for w in range(WORDS):
                    nc.tensor.transpose(
                        out=xT_ps[:, w, j * P : (j + 1) * P], in_=x_words[:, j, w : K // 2 : WORDS], identity=ident_f[:]
                    )
            kept["xT_ps", u] = xT_ps

        def group_words(u):
            grouped = work.tile([P, UNIT * PACK], BF16, align_bytes=64)
            nc.scalar.copy(
                out=grouped[:].bitcast(F32).rearrange("p (r w) -> p r w", w=WORDS),
                in_=kept["xT_ps", u][:].rearrange("p w r -> p r w"),
            )
            kept["grouped", u] = grouped

        def quantise_and_multiply(u):
            x_codes = work.tile([P, UNIT], U32, align_bytes=64)
            x_plane = work.tile([P, UNIT], U8, align_bytes=64)
            nc.vector.quantize_mx(out=x_codes[:].bitcast(FP8X4), scales=x_plane[:], in_=kept["grouped", u][:])
            if in_rows(u):
                y_rows_ps = psum.tile([P, J, D], F32, tag="yT_ps")
                for j in range(J):
                    nc.tensor.matmul_mx(
                        out=y_rows_ps[:, j, :],
                        lhsT=x_codes[:, j * P : (j + 1) * P].bitcast(FP8X4),
                        lhsT_scale=x_plane[:, j * P : (j + 1) * P],
                        rhs=wf_sb[:].bitcast(FP4X4),
                        rhs_scale=wf_plane[:],
                        start=True,
                        stop=True,
                    )
                kept["y_rows_ps", u] = y_rows_ps
                return
            yT_ps = psum.tile([P, HALVES, UNIT], F32, tag="yT_ps")
            for h in range(HALVES):
                nc.tensor.matmul_mx(
                    out=yT_ps[:, h, :],
                    lhsT=wf_sb[:, h * 2 * P : (h + 1) * 2 * P].bitcast(FP4X4),
                    lhsT_scale=wf_plane[:, h * P : (h + 1) * P],
                    rhs=x_codes[:].bitcast(FP8X4),
                    rhs_scale=x_plane[:],
                    start=True,
                    stop=True,
                )
            kept["yT_ps", u] = yT_ps

        def y_to_rows(u):
            yT = work.tile([P, HALVES, UNIT], F32)
            for h in range(HALVES):
                nc.scalar.activation(
                    out=yT[:, h, :],
                    in_=kept["yT_ps", u][:, h, :],
                    func=ACT.Identity,
                    bias=vec_cols[:, BIAS_F + h : BIAS_F + h + 1],
                )
            y_ps = psum.tile([P, J, D], F32, tag="y_ps")
            for j in range(J):
                for h in range(HALVES):
                    nc.tensor.transpose(
                        out=y_ps[:, j, h * P : (h + 1) * P], in_=yT[:, h, j * P : (j + 1) * P], identity=ident_f[:]
                    )
            kept["y_ps", u] = y_ps

        def statistics(u):
            y = work.tile([P, J, D], F32, bufs=2 + WAITING)
            y_sum = stats.tile([P, J], F32)
            for j in range(J):
                nc.scalar.activation(
                    out=y[:, j, :], in_=kept["y_ps", u][:, j, :], func=ACT.Identity, accum_out=y_sum[:, j : j + 1]
                )
            kept["y", u] = y
            kept["y_sum", u] = y_sum
            variance(u)

        def variance(u):
            y, y_sum = kept["y", u], kept["y_sum", u]
            neg_mean = stats.tile([P, J], F32)
            nc.scalar.activation(out=neg_mean[:], in_=y_sum[:], func=ACT.Copy, scale=-1.0 / D)
            kept["neg_mean", u] = neg_mean
            squares_and_rstd(u)

        def squares_and_rstd(u):
            y, neg_mean = kept["y", u], kept["neg_mean", u]
            sq_sum = stats.tile([P, J], F32)
            for j in range(J):
                squares = work.tile([P, D], BF16, tag="unused")
                nc.scalar.activation(
                    out=squares[:],
                    in_=y[:, j, :],
                    func=ACT.Square,
                    bias=neg_mean[:, j : j + 1],
                    accum_out=sq_sum[:, j : j + 1],
                )
            var_eps = stats.tile([P, J], F32)
            nc.scalar.activation(out=var_eps[:], in_=sq_sum[:], func=ACT.Copy, scale=1.0 / D, bias=LN_EPS)
            rstd = stats.tile([P, J], F32)
            nc.gpsimd.tensor_tensor(out=rstd[:], in0=var_eps[:], in1=minus_half[:], op=ALU.pow)
            kept["rstd", u] = rstd

        def z_to_columns(u):
            z_rows(u)
            z_transposes(u)

        def z_rows(u):
            y, neg_mean, rstd = kept["y", u], kept["neg_mean", u], kept["rstd", u]
            shift = stats.tile([P, J], F32)
            z = work.tile([P, J, D], F32)
            for j in range(J):
                nc.scalar.activation(
                    out=shift[:, j : j + 1], in_=neg_mean[:, j : j + 1], func=ACT.Copy, scale=rstd[:, j : j + 1]
                )
            for j in range(J):
                nc.scalar.activation(
                    out=z[:, j, :], in_=y[:, j, :], func=ACT.Identity, scale=rstd[:, j : j + 1], bias=shift[:, j : j + 1]
                )
            kept["z", u] = z

        def z_transposes(u):
            z = kept["z", u]
            zT_ps = psum.tile([P, HALVES, UNIT], F32, tag="zT_ps")
            for h in range(HALVES):
                for j in range(J):
                    nc.tensor.transpose(
                        out=zT_ps[:, h, j * P : (j + 1) * P], in_=z[:, j, h * P : (h + 1) * P], identity=ident_f[:]
                    )
            kept["zT_ps", u] = zT_ps

        def gelu_to_rows(u):
            geluT = work.tile([P, HALVES, UNIT], F32)
            for h in range(HALVES):
                nc.scalar.activation(
                    out=geluT[:, h, :],
                    in_=kept["zT_ps", u][:, h, :],
                    func=ACT.Gelu,
                    scale=vec_cols[:, LN_G + h : LN_G + h + 1],
                    bias=vec_cols[:, LN_B + h : LN_B + h + 1],
                )
            gelu_ps = psum.tile([P, J, D], F32, tag="hT_then_gelu", bufs=2)
            for j in range(J):
                for h in range(HALVES):
                    nc.tensor.transpose(
                        out=gelu_ps[:, j, h * P : (h + 1) * P], in_=geluT[:, h, j * P : (j + 1) * P], identity=ident_f[:]
                    )
            kept["gelu_ps", u] = gelu_ps

        def finish(u):
            result = work.tile([P, J, D], F32)
            for j in range(J):
                col = u * J + j
                nc.vector.scalar_tensor_tensor(
                    out=result[:, j, :],
                    in0=kept["gelu_ps", u][:, j, :],
                    scalar=af_factor[:, col : col + 1],
                    in1=kept["x", u][:, j, 0:D],
                    op0=ALU.mult,
                    op1=ALU.add,
                )
            nc.sync.dma_start(out=out_units[u], in_=result[:].rearrange("p j d -> p (j d)"))

        def group_and_quantise(u, j):
            if j == 0:
                grouped = work.tile([P, UNIT * PACK], BF16, align_bytes=64)
                x_codes = work.tile([P, UNIT], U32, align_bytes=64)
                x_plane = work.tile([P, UNIT], U8, align_bytes=64)
                kept["grouped", u], kept["x_codes", u], kept["x_plane", u] = grouped, x_codes, x_plane
            grouped, x_codes, x_plane = kept["grouped", u], kept["x_codes", u], kept["x_plane", u]
            nc.scalar.copy(
                out=grouped[:, j * P * PACK : (j + 1) * P * PACK].bitcast(F32).rearrange("p (r w) -> p r w", w=WORDS),
                in_=kept["xT_ps", u][:, :, j * P : (j + 1) * P].rearrange("p w r -> p r w"),
            )
            nc.vector.quantize_mx(
                out=x_codes[:, j * P : (j + 1) * P].bitcast(FP8X4),
                scales=x_plane[:, j * P : (j + 1) * P],
                in_=grouped[:, j * P * PACK : (j + 1) * P * PACK],
            )

        def multiply_rows(u, j):
            if j == 0:
                y_rows_ps = psum.tile([P, J, D], F32, tag="yT_ps")
                kept["y_rows_ps", u] = y_rows_ps
            nc.tensor.matmul_mx(
                out=kept["y_rows_ps", u][:, j, :],
                lhsT=kept["x_codes", u][:, j * P : (j + 1) * P].bitcast(FP8X4),
                lhsT_scale=kept["x_plane", u][:, j * P : (j + 1) * P],
                rhs=wf_sb[:].bitcast(FP4X4),
                rhs_scale=wf_plane[:],
                start=True,
                stop=True,
            )

        def add_bias_rows(u, j):
            if j == 0:
                y = work.tile([P, J, D], F32, bufs=2 + WAITING)
                y_sum = stats.tile([P, J], F32)
                kept["y", u], kept["y_sum", u] = y, y_sum
            nc.vector.scalar_tensor_tensor(
                out=kept["y", u][:, j, :],
                in0=kept["y_rows_ps", u][:, j, :],
                scalar=1.0,
                in1=kept["row_vecs"][:, 0, :],
                op0=ALU.mult,
                op1=ALU.add,
                accum_out=kept["y_sum", u][:, j : j + 1],
            )

        def negate_mean(u):
            neg_mean = stats.tile([P, J], F32)
            nc.vector.tensor_scalar_mul(out=neg_mean[:], in0=kept["y_sum", u][:], scalar1=-1.0 / D)
            kept["neg_mean", u] = neg_mean

        def centre_rows(u):
            centred = work.tile([P, J, D], F32)
            for j in range(J):
                nc.vector.scalar_tensor_tensor(
                    out=centred[:, j, :],
                    in0=kept["y", u][:, j, :],
                    scalar=kept["neg_mean", u][:, j : j + 1],
                    in1=kept["row_vecs"][:, 1, :],
                    op0=ALU.add,
                    op1=ALU.mult,
                )
            kept["centred", u] = centred

        def normalise_rows(u):
            yn = work.tile([P, J, D], F32)
            for j in range(J):
                nc.vector.scalar_tensor_tensor(
                    out=yn[:, j, :],
                    in0=kept["centred", u][:, j, :],
                    scalar=kept["rstd", u][:, j : j + 1],
                    in1=kept["row_vecs"][:, 2, :],
                    op0=ALU.mult,
                    op1=ALU.add,
                )
            kept["yn", u] = yn

        def gelu_rows(u):
            gelu_sb = work.tile([P, J, D], F32)
            for j in range(J):
                nc.scalar.activation(out=gelu_sb[:, j, :], in_=kept["yn", u][:, j, :], func=ACT.Gelu)
            kept["gelu_ps", u] = gelu_sb

        def run(stage, u):
            if 0 <= u < UNITS:
                stage(u)

        h_to_columns(0)
        chunks_done = 0
        norm_step = norm_steps()
        for i in range(UNITS):
            normed = [u for u in sorted(norm_step) if norm_step[u] == i]
            before = [u for u in sorted(norm_step) if norm_step[u] == i - 1]
            rows_now = i - 2 in EARLY_ROW_UNITS
            run(load_unit, i + PREFETCH)
            if rows_now:
                add_bias_rows(i - 2, 0)
                add_bias_rows(i - 2, 1)
                negate_mean(i - 2)
            run(pool_wide, i)
            run(x_to_columns, i - 1)
            if rows_now:
                squares_and_rstd(i - 2)
            else:
                run(y_to_rows, i - 2)
            for u in normed[:1]:
                z_to_columns(u)
            run(group_words, i - 1)
            for c in range(chunks_done, chunks_done + (CHUNK_PLAN[i] if i < len(CHUNK_PLAN) else 0)):
                if c + 1 < CHUNKS:
                    h_to_columns(c + 1)
                gate_chunk(c)
                chunks_done = c + 1
            if rows_now:
                centre_rows(i - 2)
            else:
                run(statistics, i - 2)
            early = before[: max(0, len(before) + len(normed) - 2)]
            for u in early[:1]:
                finish(u)
            for u in normed[:1]:
                gelu_to_rows(u)
            for u in normed[1:]:
                z_to_columns(u)
            run(quantise_and_multiply, i - 1)
            if i - LAST_LAG in EARLY_ROW_UNITS:
                normalise_rows(i - LAST_LAG)
            for u in EARLY_ROW_UNITS:
                if max(u + LAST_LAG, FIRST_GELU) == i:
                    gelu_rows(u)
            for u in early[1:]:
                finish(u)
            for u in normed[1:]:
                gelu_to_rows(u)
            run(pool_narrow, i)
            if i == UNITS - 1:
                mix_sum_and_max(i)
            for u in before[len(early) :]:
                finish(u)
            if i < UNITS - 1:
                mix_sum_and_max(i)
            for u in EARLY_ROW_UNITS:
                if max(u + LAST_LAG, FIRST_GELU) == i - 1:
                    finish(u)
        assert chunks_done == CHUNKS

        assert ROW_UNITS == 2 and LAST_LAG == 3
        last = UNITS - 1
        x_to_columns(last)
        add_bias_rows(last - 1, 0)
        add_bias_rows(last - 1, 1)
        negate_mean(last - 1)
        z_rows(last - 2)
        finish(last - 3)
        group_and_quantise(last, 0)
        multiply_rows(last, 0)
        squares_and_rstd(last - 1)
        centre_rows(last - 1)
        z_transposes(last - 2)
        group_and_quantise(last, 1)
        multiply_rows(last, 1)
        add_bias_rows(last, 0)
        gelu_to_rows(last - 2)
        normalise_rows(last - 1)
        add_bias_rows(last, 1)
        negate_mean(last)
        gelu_rows(last - 1)
        squares_and_rstd(last)
        centre_rows(last)
        finish(last - 1)
        normalise_rows(last)
        finish(last - 2)
        gelu_rows(last)
        finish(last)
